import numpy as np
import ml_dtypes


def mxq(x, axis, fmt="e4m3"):
    dtype, down = {"e4m3": (ml_dtypes.float8_e4m3fn, 7), "e5m2": (ml_dtypes.float8_e5m2, 14)}[fmt]
    v = np.moveaxis(np.asarray(x, np.float32).astype(ml_dtypes.bfloat16).astype(np.float64), axis, -1)
    blocks = v.reshape(v.shape[:-1] + (-1, 32))
    amax = np.abs(blocks).max(-1, keepdims=True)
    byte = np.maximum(np.where(amax > 0, np.frexp(amax)[1] - 1 + 127, 0) - down, 1)
    scale = np.exp2(byte - 127.0)
    codes = (blocks / scale).astype(np.float32).astype(dtype).astype(np.float64)
    return np.moveaxis((codes * scale).reshape(v.shape), -1, axis)


WIDE = False


def mx_kscale(k):
    if not WIDE:
        return np.ones(k)
    levels = np.array([10, -10, 5, -5, 0])
    a = np.random.permutation(np.resize(levels, k // 512 * 4)).reshape(k // 512, 4)
    idx = np.arange(k)
    return np.exp2(a[idx // 512, idx % 128 // 32])


BF16 = ml_dtypes.bfloat16


def bf(x):
    return np.asarray(x, np.float32).astype(BF16)


def f64(x):
    return np.asarray(x).astype(np.float64)


E2M1 = np.array([0.0, 0.5, 1.0, 1.5, 2.0, 3.0, 4.0, 6.0, -0.0, -0.5, -1.0, -1.5, -2.0, -3.0, -4.0, -6.0])


def pack_weight(w, fmt):
    k, n = w.shape
    w = f64(bf(w)).reshape(k // 32, 32, n)
    amax = np.abs(w).max(1)
    if fmt == "e4m3":
        byte = np.frexp(amax)[1] - 1 + 127 - 7
    else:
        mant, ex = np.frexp(amax / 6.0)
        byte = np.where(mant > 0.5, ex, ex - 1) + 127
    byte = np.clip(np.where(amax > 0, byte, 1), 1, 254)
    scaled = (w * np.exp2(127.0 - byte)[:, None, :]).reshape(k, n).astype(np.float32)
    by_word = np.ascontiguousarray(scaled.reshape(k // 512, 128, 4, n).transpose(0, 1, 3, 2))
    if fmt == "e4m3":
        words = by_word.astype(ml_dtypes.float8_e4m3fn).view(np.uint8)
    else:
        c = by_word.astype(ml_dtypes.float4_e2m1fn).view(np.uint8) & 0xF
        words = c[..., 0::2] | (c[..., 1::2] << 4)
    return np.ascontiguousarray(words), np.ascontiguousarray(byte.astype(np.uint8).reshape(k // 512, 16, n))


def unpack_weight(words, scales, fmt):
    g, p, n, _ = words.shape
    if fmt == "e4m3":
        vals = np.ascontiguousarray(words).view(ml_dtypes.float8_e4m3fn).astype(np.float64)
    else:
        nib = np.empty((g, p, n, 4), np.uint8)
        nib[..., 0::2] = words & 0xF
        nib[..., 1::2] = words >> 4
        vals = E2M1[nib]
    vals = vals * np.repeat(np.exp2(scales.astype(np.float64) - 127.0), 8, axis=1)[..., None]
    return vals.transpose(0, 1, 3, 2).reshape(g * 512, n)


B, STOCH, ACT_DIM, HIDDEN, DETER = 256, 1024, 512, 2048, 2048
EPS = 1e-4
DT_MIN = 1e-4
FMT = "e4m3"


def softplus(v):
    return np.maximum(v, 0.0) + np.log1p(np.exp(-np.abs(v)))


def sigmoid(v):
    return 1.0 / (1.0 + np.exp(-v))


def rmsnorm(v, w):
    return v * (1.0 / np.sqrt(np.mean(v * v, axis=-1, keepdims=True) + EPS)) * w


def setup_inputs():
    s = mx_kscale(DETER)
    r = np.maximum(s, 1.0)

    def w():
        return np.random.standard_normal((DETER, DETER)) / np.sqrt(DETER) / s

    def bias():
        return np.random.standard_normal(DETER) * 0.2

    x = bf(np.random.standard_normal((B, DETER)) * 0.9 * s)
    deter = bf(np.random.standard_normal((B, DETER)))
    a_base = bf(np.random.standard_normal(DETER))
    dt_w_words, dt_w_scales = pack_weight(np.ascontiguousarray(w().T), FMT)
    dt_b = bf(bias())
    b_w_words, b_w_scales = pack_weight(np.ascontiguousarray(w().T), FMT)
    b_b = bf(bias())
    c_w_words, c_w_scales = pack_weight(np.ascontiguousarray((w() / r[:, None]).T), FMT)
    c_b = bf(bias() / r)
    z_w_words, z_w_scales = pack_weight(np.ascontiguousarray(w().T), FMT)
    z_b = bf(bias())
    skip = bf(np.random.standard_normal(DETER) * 0.5 / s)
    norm_w = bf(1.0 + 0.1 * np.random.standard_normal(DETER))
    return {"x": x,
            "deter": deter,
            "a_base": a_base,
            "dt_w_words": dt_w_words, "dt_w_scales": dt_w_scales, "dt_b": dt_b,
            "b_w_words": b_w_words, "b_w_scales": b_w_scales, "b_b": b_b,
            "c_w_words": c_w_words, "c_w_scales": c_w_scales, "c_b": c_b,
            "z_w_words": z_w_words, "z_w_scales": z_w_scales, "z_b": z_b,
            "skip": skip,
            "norm_w": norm_w}


def reference(x, deter, a_base, dt_w_words, dt_w_scales, dt_b, b_w_words, b_w_scales, b_b, c_w_words, c_w_scales, c_b, z_w_words, z_w_scales, z_b, skip, norm_w):
    x, deter = f64(x), f64(deter)
    xq = mxq(x, 1, "e4m3")
    dt = softplus((xq @ unpack_weight(dt_w_words, dt_w_scales, FMT)) + f64(dt_b)) + DT_MIN
    a = -softplus(f64(a_base))
    b = np.tanh((xq @ unpack_weight(b_w_words, b_w_scales, FMT)) + f64(b_b))
    c = (xq @ unpack_weight(c_w_words, c_w_scales, FMT)) + f64(c_b)
    z = sigmoid((xq @ unpack_weight(z_w_words, z_w_scales, FMT)) + f64(z_b))
    state = np.exp(a * dt) * deter + dt * b * x
    y = c * state + f64(skip) * x
    out = z * y + (1.0 - z) * deter
    return rmsnorm(out, f64(norm_w))

@@ -1,0 +1,476 @@
+from contextlib import ExitStack
+
+import concourse.mybir as mybir
+from concourse.masks import make_identity
+
+F32 = mybir.dt.float32
+BF16 = mybir.dt.bfloat16
+I32 = mybir.dt.int32
+U32 = mybir.dt.uint32
+U8 = mybir.dt.uint8
+FP8X4 = mybir.dt.float8_e4m3fn_x4
+ACT = mybir.ActivationFunctionType
+ALU = mybir.AluOpType
+
+P = 128
+PACK = 4
+TOKENS = 256
+TOKEN_TILES = TOKENS // P
+CHANNELS = 2048
+GROUPS = CHANNELS // (P * PACK)
+CH_TILES = CHANNELS // P
+BLOCK_TILES = 4
+BLOCKS = CH_TILES // BLOCK_TILES
+BLOCK_CH = BLOCK_TILES * P
+HALF_TILES = 2
+HALVES = BLOCK_TILES // HALF_TILES
+WORDS_PER_GROUP = P * PACK // 2
+
+WEIGHT_BUFS = 12
+DT_BANKS = 2
+ACC_BANKS = 6
+
+DT_MIN = 1e-4
+EPS = 1e-4
+LN_MAX = 1e18
+
+DT_B, B_B, C_B, Z_B, A_BASE, SKIP = 0, 1, 2, 3, 4, 5
+VECTOR_ROWS = 6 * CH_TILES
+
+FLOPS = 2 * TOKENS * CHANNELS * CHANNELS * 4
+
+
+def tile_mamba2backbone_pb_kernel(
+    tc,
+    x,
+    deter,
+    a_base,
+    dt_w_words,
+    dt_w_scales,
+    dt_b,
+    b_w_words,
+    b_w_scales,
+    b_b,
+    c_w_words,
+    c_w_scales,
+    c_b,
+    z_w_words,
+    z_w_scales,
+    z_b,
+    skip,
+    norm_w,
+    out,
+):
+    nc = tc.nc
+    weight_words = {"dt": dt_w_words, "b": b_w_words, "c": c_w_words, "z": z_w_words}
+    weight_scales = {"dt": dt_w_scales, "b": b_w_scales, "c": c_w_scales, "z": z_w_scales}
+    weight_index = {"dt": 0, "b": 1, "c": 2, "z": 3}
+
+    pieces = [("dt", 0)]
+    for j in range(BLOCKS):
+        pieces.append(("b", j))
+        if j + 1 < BLOCKS:
+            pieces.append(("dt", j + 1))
+        pieces.append(("c", j))
+        pieces.append(("z", j))
+
+    with ExitStack() as stack:
+        stack.enter_context(tc.manual_schedule())
+        keep = stack.enter_context(tc.tile_pool(name="keep", bufs=1))
+        weights = stack.enter_context(tc.tile_pool(name="weights", bufs=WEIGHT_BUFS))
+        work = stack.enter_context(tc.tile_pool(name="work", bufs=2))
+        psum = stack.enter_context(tc.psum_pool(name="psum", bufs=ACC_BANKS))
+
+        ident_bf16 = keep.tile([P, P], BF16)
+        ident_f32 = keep.tile([P, P], F32)
+        vector_rows = keep.tile([P, P], BF16)
+        per_channel = keep.tile([P, P], F32)
+        half_z_b = keep.tile([P, CH_TILES], F32)
+        soft_a = keep.tile([P, CH_TILES], F32)
+        a_neg = keep.tile([P, CH_TILES], F32)
+        a_dt_min = keep.tile([P, CH_TILES], F32)
+        one = keep.tile([P, 1], F32)
+        minus_half = keep.tile([P, TOKEN_TILES], F32)
+        x_rows = keep.tile([P, TOKEN_TILES, CHANNELS], BF16)
+        deter_rows = keep.tile([P, TOKEN_TILES, CHANNELS], BF16)
+        x_grouped = keep.tile([P, GROUPS, TOKENS * PACK], BF16, align_bytes=64)
+        x_codes = keep.tile([P, GROUPS, TOKENS], U32, align_bytes=64)
+        x_planes = keep.tile([P, GROUPS, TOKENS], U8, align_bytes=64)
+        w_planes = keep.tile([P, len(weight_index), CHANNELS], U8, align_bytes=64)
+        x_t = keep.tile([P, CH_TILES, TOKENS], BF16)
+        deter_t = keep.tile([P, CH_TILES, TOKENS], BF16)
+        skip_x = keep.tile([P, CH_TILES, TOKENS], F32)
+        blended = keep.tile([P, TOKEN_TILES, CHANNELS], F32)
+        norm_w_all = keep.tile([P, CHANNELS], BF16)
+        squares = keep.tile([P, TOKEN_TILES, BLOCKS], F32)
+        mean_sq = keep.tile([P, TOKEN_TILES], F32)
+        rstd = keep.tile([P, TOKEN_TILES], F32)
+
+        def channel_scalar(vector, ct):
+            column = CH_TILES * vector + ct
+            return per_channel[:, column : column + 1]
+
+        for v, vector in enumerate((dt_b, b_b, c_b, z_b, a_base, skip)):
+            nc.scalar.dma_start(
+                out=vector_rows[CH_TILES * v : CH_TILES * (v + 1), :],
+                in_=vector.rearrange("(r c) -> r c", c=P),
+            )
+        nc.vector.memset(vector_rows[VECTOR_ROWS:P, :], 0.0)
+
+        nc.vector.memset(w_planes[:].bitcast(I32), 0)
+        nc.vector.memset(one[:], 1.0)
+
+        piece_tiles = {}
+
+        def load_piece(k):
+            name, j = pieces[k]
+            if j == 0:
+                for quadrant in range(4):
+                    nc.sync.dma_start(
+                        out=w_planes[32 * quadrant : 32 * quadrant + 16, weight_index[name], :].bitcast(I32),
+                        in_=weight_scales[name][:, 4 * quadrant : 4 * quadrant + 4, :].bitcast(I32),
+                    )
+            piece = weights.tile([P, GROUPS, BLOCK_CH], U32, align_bytes=64, tag="piece", name="piece")
+            by_partition = weight_words[name].rearrange("g p n t -> p g (n t)")
+            nc.sync.dma_start(
+                out=piece[:].bitcast(I32),
+                in_=by_partition[:, :, PACK * BLOCK_CH * j : PACK * BLOCK_CH * (j + 1)].bitcast(I32),
+            )
+            piece_tiles[k] = piece
+
+        for t in range(TOKEN_TILES):
+            nc.sync.dma_start(out=x_rows[:, t, :], in_=x[t * P : (t + 1) * P, :])
+        for t in range(TOKEN_TILES):
+            nc.sync.dma_start(out=deter_rows[:, t, :], in_=deter[t * P : (t + 1) * P, :])
+        for k in range(WEIGHT_BUFS):
+            load_piece(k)
+
+        make_identity(nc, ident_bf16[:])
+        make_identity(nc, ident_f32[:])
+        nc.gpsimd.memset(minus_half[:], -0.5)
+
+        def multiply(name, j):
+            k = pieces.index((name, j))
+            piece = piece_tiles[k]
+            banks = []
+            for h in range(HALVES):
+                if name == "dt":
+                    bank = psum.tile([P, HALF_TILES, TOKENS], F32, tag="dt", bufs=DT_BANKS, name="dt_bank")
+                else:
+                    bank = psum.tile([P, HALF_TILES, TOKENS], F32, tag="acc", name="bank")
+                for i in range(HALF_TILES):
+                    local = (h * HALF_TILES + i) * P
+                    channel = j * BLOCK_CH + local
+                    for g in range(GROUPS):
+                        nc.tensor.matmul_mx(
+                            out=bank[:, i, :],
+                            lhsT=piece[:, g, local : local + P].bitcast(FP8X4),
+                            lhsT_scale=w_planes[4 * g : P, weight_index[name], channel : channel + P],
+                            rhs=x_codes[:, g, :].bitcast(FP8X4),
+                            rhs_scale=x_planes[:, g, :],
+                            start=(g == 0),
+                            stop=(g == GROUPS - 1),
+                        )
+                banks.append(bank)
+            if k + WEIGHT_BUFS < len(pieces):
+                load_piece(k + WEIGHT_BUFS)
+            return banks
+
+        def tiles_of(j):
+            return [(i, i // HALF_TILES, i % HALF_TILES, j * BLOCK_TILES + i) for i in range(BLOCK_TILES)]
+
+        def half_slices(j):
+            return [
+                (
+                    slice(h * HALF_TILES, (h + 1) * HALF_TILES),
+                    slice(j * BLOCK_TILES + h * HALF_TILES, j * BLOCK_TILES + (h + 1) * HALF_TILES),
+                )
+                for h in range(HALVES)
+            ]
+
+        def quantise(g):
+            nc.vector.quantize_mx(
+                out=x_codes[:, g, :].bitcast(FP8X4), scales=x_planes[:, g, :], in_=x_grouped[:, g, :]
+            )
+
+        pairs = [psum.tile([P, 2, TOKENS], F32, tag="acc", name="pairs") for g in range(GROUPS)]
+        for t in range(TOKEN_TILES):
+            for g in range(GROUPS):
+                for u in range(2):
+                    nc.tensor.transpose(
+                        pairs[g][:, u, t * P : (t + 1) * P],
+                        x_rows[:, t, :].bitcast(F32)[
+                            :, WORDS_PER_GROUP * g + u : WORDS_PER_GROUP * (g + 1) : 2
+                        ],
+                        ident_f32[:],
+                    )
+        for g in range(GROUPS):
+            nc.vector.tensor_copy(
+                out=x_grouped[:, g, :].bitcast(F32).rearrange("p (r u) -> p r u", u=2),
+                in_=pairs[g][:].rearrange("p u r -> p r u"),
+            )
+            if g > 0:
+                quantise(g - 1)
+        quantise(GROUPS - 1)
+
+        vector_cols = psum.tile([P, P], BF16, tag="acc", name="vector_cols")
+        nc.tensor.transpose(vector_cols[:], vector_rows[:], ident_bf16[:])
+        nc.scalar.copy(out=per_channel[:], in_=vector_cols[:])
+        a_base_cols = per_channel[:, CH_TILES * A_BASE : CH_TILES * (A_BASE + 1)]
+        nc.scalar.activation(out=soft_a[:], in_=a_base_cols, func=ACT.Exp)
+
+        nc.vector.tensor_scalar_mul(
+            out=half_z_b[:], in0=per_channel[:, CH_TILES * Z_B : CH_TILES * (Z_B + 1)], scalar1=0.5
+        )
+        nc.vector.tensor_scalar_min(out=soft_a[:], in0=soft_a[:], scalar1=LN_MAX)
+
+        def transpose_rows(rows, pair):
+            flipped = psum.tile([P, HALF_TILES, TOKENS], BF16, tag="acc", name="flipped")
+            for i in range(HALF_TILES):
+                ct = pair * HALF_TILES + i
+                for t in range(TOKEN_TILES):
+                    nc.tensor.transpose(
+                        flipped[:, i, t * P : (t + 1) * P], rows[:, t, ct * P : (ct + 1) * P], ident_bf16[:]
+                    )
+            return flipped
+
+        for rows, rows_t in ((x_rows, x_t), (deter_rows, deter_t)):
+            for pair in range(CH_TILES // HALF_TILES):
+                flipped = transpose_rows(rows, pair)
+                nc.scalar.copy(out=rows_t[:, pair * HALF_TILES : (pair + 1) * HALF_TILES, :], in_=flipped[:])
+
+        dt_banks, b_banks, c_banks, z_banks, back_banks = {}, {}, {}, {}, {}
+        soft, decay, chain, gate = {}, {}, {}, {}
+
+        def softplus_exp(j):
+            soft[j] = work.tile([P, BLOCK_TILES, TOKENS], F32, tag="soft", name="soft")
+            for i, h, ih, ct in tiles_of(j):
+                nc.scalar.activation(
+                    out=soft[j][:, i, :], in_=dt_banks[j][h][:, ih, :], func=ACT.Exp, bias=channel_scalar(DT_B, ct)
+                )
+
+        def softplus_cut(j):
+            for mine, whole in half_slices(j):
+                nc.vector.tensor_scalar_min(out=soft[j][:, mine, :], in0=soft[j][:, mine, :], scalar1=LN_MAX)
+
+        def softplus_log(j):
+            for mine, whole in half_slices(j):
+                nc.scalar.activation(out=soft[j][:, mine, :], in_=soft[j][:, mine, :], func=ACT.Ln, bias=one[:])
+
+        def softplus_max(j):
+            for i, h, ih, ct in tiles_of(j):
+                nc.vector.scalar_tensor_tensor(
+                    out=soft[j][:, i, :],
+                    in0=dt_banks[j][h][:, ih, :],
+                    scalar=channel_scalar(DT_B, ct),
+                    in1=soft[j][:, i, :],
+                    op0=ALU.add,
+                    op1=ALU.max,
+                )
+
+        def decay_exp(j):
+            decay[j] = work.tile([P, BLOCK_TILES, TOKENS], F32, tag="decay", name="decay")
+            for i, h, ih, ct in tiles_of(j):
+                nc.scalar.activation(
+                    out=decay[j][:, i, :],
+                    in_=soft[j][:, i, :],
+                    func=ACT.Exp,
+                    scale=a_neg[:, ct : ct + 1],
+                    bias=a_dt_min[:, ct : ct + 1],
+                )
+
+        def skip_term(j):
+            for i, h, ih, ct in tiles_of(j):
+                nc.vector.scalar_tensor_tensor(
+                    out=skip_x[:, ct, :],
+                    in0=x_t[:, ct, :],
+                    scalar=channel_scalar(SKIP, ct),
+                    in1=deter_t[:, ct, :],
+                    op0=ALU.mult,
+                    op1=ALU.subtract,
+                )
+
+        def tanh_b(j):
+            chain[j] = work.tile([P, BLOCK_TILES, TOKENS], F32, tag="chain", name="chain")
+            for i, h, ih, ct in tiles_of(j):
+                nc.scalar.activation(
+                    out=chain[j][:, i, :], in_=b_banks[j][h][:, ih, :], func=ACT.Tanh, bias=channel_scalar(B_B, ct)
+                )
+
+        def tanh_z(j):
+            gate[j] = work.tile([P, BLOCK_TILES, TOKENS], F32, tag="gate", name="gate")
+            for i, h, ih, ct in tiles_of(j):
+                nc.scalar.activation(
+                    out=gate[j][:, i, :],
+                    in_=z_banks[j][h][:, ih, :],
+                    func=ACT.Tanh,
+                    scale=0.5,
+                    bias=half_z_b[:, ct : ct + 1],
+                )
+
+        def decay_times_deter(j):
+            for mine, whole in half_slices(j):
+                nc.vector.tensor_tensor(
+                    out=decay[j][:, mine, :], in0=decay[j][:, mine, :], in1=deter_t[:, whole, :], op=ALU.mult
+                )
+
+        def b_times_x(j):
+            for mine, whole in half_slices(j):
+                nc.vector.tensor_tensor(
+                    out=chain[j][:, mine, :], in0=chain[j][:, mine, :], in1=x_t[:, whole, :], op=ALU.mult
+                )
+
+        def times_dt(j):
+            for mine, whole in half_slices(j):
+                nc.vector.scalar_tensor_tensor(
+                    out=chain[j][:, mine, :],
+                    in0=soft[j][:, mine, :],
+                    scalar=DT_MIN,
+                    in1=chain[j][:, mine, :],
+                    op0=ALU.add,
+                    op1=ALU.mult,
+                )
+
+        def new_state(j):
+            for mine, whole in half_slices(j):
+                nc.vector.tensor_tensor(
+                    out=chain[j][:, mine, :], in0=chain[j][:, mine, :], in1=decay[j][:, mine, :], op=ALU.add
+                )
+
+        def times_c(j):
+            for i, h, ih, ct in tiles_of(j):
+                nc.vector.scalar_tensor_tensor(
+                    out=chain[j][:, i, :],
+                    in0=c_banks[j][h][:, ih, :],
+                    scalar=channel_scalar(C_B, ct),
+                    in1=chain[j][:, i, :],
+                    op0=ALU.add,
+                    op1=ALU.mult,
+                )
+
+        def plus_skip_term(j):
+            for mine, whole in half_slices(j):
+                nc.vector.tensor_tensor(
+                    out=chain[j][:, mine, :], in0=chain[j][:, mine, :], in1=skip_x[:, whole, :], op=ALU.add
+                )
+
+        def times_gate(j):
+            for mine, whole in half_slices(j):
+                nc.vector.scalar_tensor_tensor(
+                    out=chain[j][:, mine, :],
+                    in0=gate[j][:, mine, :],
+                    scalar=1.0,
+                    in1=chain[j][:, mine, :],
+                    op0=ALU.add,
+                    op1=ALU.mult,
+                )
+
+        def transpose_back(j):
+            back_banks[j] = []
+            for t in range(TOKEN_TILES):
+                back = psum.tile([P, BLOCK_CH], F32, tag="acc", name="back")
+                for i in range(BLOCK_TILES):
+                    nc.tensor.transpose(
+                        back[:, i * P : (i + 1) * P], chain[j][:, i, t * P : (t + 1) * P], ident_f32[:]
+                    )
+                back_banks[j].append(back)
+
+        def blend(j):
+            for t in range(TOKEN_TILES):
+                nc.vector.scalar_tensor_tensor(
+                    out=blended[:, t, j * BLOCK_CH : (j + 1) * BLOCK_CH],
+                    in0=back_banks[j][t][:],
+                    scalar=0.5,
+                    in1=deter_rows[:, t, j * BLOCK_CH : (j + 1) * BLOCK_CH],
+                    op0=ALU.mult,
+                    op1=ALU.add,
+                )
+
+        def sum_squares(j):
+            for t in range(TOKEN_TILES):
+                unread = work.tile([P, BLOCK_CH], F32, tag="unread", name="unread")
+                nc.scalar.activation(
+                    out=unread[:],
+                    in_=blended[:, t, j * BLOCK_CH : (j + 1) * BLOCK_CH],
+                    func=ACT.Square,
+                    accum_out=squares[:, t, j : j + 1],
+                )
+
+        dt_banks[0] = multiply("dt", 0)
+        softplus_exp(0)
+        for j in range(BLOCKS - 1):
+            skip_term(j)
+        softplus_cut(0)
+        skip_term(BLOCKS - 1)
+        nc.scalar.activation(out=soft_a[:], in_=soft_a[:], func=ACT.Ln, bias=one[:])
+        softplus_log(0)
+        nc.vector.tensor_tensor(out=soft_a[:], in0=soft_a[:], in1=a_base_cols, op=ALU.max)
+        nc.vector.tensor_scalar_mul(out=a_neg[:], in0=soft_a[:], scalar1=-1.0)
+        nc.vector.tensor_scalar_mul(out=a_dt_min[:], in0=soft_a[:], scalar1=-DT_MIN)
+        softplus_max(0)
+        decay_exp(0)
+        b_banks[0] = multiply("b", 0)
+        dt_banks[1] = multiply("dt", 1)
+
+        for j in range(BLOCKS):
+            more = j + 1 < BLOCKS
+            c_banks[j] = multiply("c", j)
+            tanh_b(j)
+            z_banks[j] = multiply("z", j)
+            if j == 1:
+                nc.sync.dma_start(out=norm_w_all[:], in_=norm_w.partition_broadcast(P))
+            decay_times_deter(j)
+            if j > 0:
+                blend(j - 1)
+            b_times_x(j)
+            if more:
+                softplus_exp(j + 1)
+                softplus_cut(j + 1)
+            if j > 0:
+                sum_squares(j - 1)
+            if more:
+                softplus_log(j + 1)
+            times_dt(j)
+            new_state(j)
+            times_c(j)
+            if more:
+                softplus_max(j + 1)
+            tanh_z(j)
+            if more:
+                decay_exp(j + 1)
+            plus_skip_term(j)
+            times_gate(j)
+            if more:
+                b_banks[j + 1] = multiply("b", j + 1)
+            if j + 2 < BLOCKS:
+                dt_banks[j + 2] = multiply("dt", j + 2)
+            transpose_back(j)
+        blend(BLOCKS - 1)
+        sum_squares(BLOCKS - 1)
+
+        for t in range(TOKEN_TILES):
+            mine = slice(t, t + 1)
+            nc.vector.tensor_reduce(
+                out=mean_sq[:, mine], in_=squares[:, t, :], axis=mybir.AxisListType.X, op=ALU.add
+            )
+            nc.vector.tensor_scalar(
+                out=mean_sq[:, mine],
+                in0=mean_sq[:, mine],
+                scalar1=1.0 / CHANNELS,
+                scalar2=EPS,
+                op0=ALU.mult,
+                op1=ALU.add,
+            )
+            nc.gpsimd.tensor_tensor(out=rstd[:, mine], in0=mean_sq[:, mine], in1=minus_half[:, mine], op=ALU.pow)
+        for t in range(TOKEN_TILES):
+            for j in range(BLOCKS):
+                columns = slice(j * BLOCK_CH, (j + 1) * BLOCK_CH)
+                nc.vector.scalar_tensor_tensor(
+                    out=blended[:, t, columns],
+                    in0=blended[:, t, columns],
+                    scalar=rstd[:, t : t + 1],
+                    in1=norm_w_all[:, columns],
+                    op0=ALU.mult,
+                    op1=ALU.mult,
+                )
+                nc.sync.dma_start(out=out[t * P : (t + 1) * P, columns], in_=blended[:, t, columns])

@@ -122,7 +122,24 @@ def tile_mamba2backbone_pb_kernel(
 
         piece_tiles = {}
 
+        LAST_PIECE = len(pieces) - 1
+        LOADS = LAST_PIECE + HALVES
+        piece_tiles[LAST_PIECE] = []
+
+        def load_half_piece(h):
+            name, j = pieces[LAST_PIECE]
+            by_partition = weight_words[name].rearrange("g p n t -> p g (n t)")
+            half = weights.tile([P, GROUPS, HALF_TILES * P], U32, align_bytes=64, tag="piece", name="half_piece")
+            first = PACK * (BLOCK_CH * j + HALF_TILES * P * h)
+            nc.sync.dma_start(
+                out=half[:].bitcast(I32), in_=by_partition[:, :, first : first + PACK * HALF_TILES * P].bitcast(I32)
+            )
+            piece_tiles[LAST_PIECE].append(half)
+
         def load_piece(k):
+            if k >= LAST_PIECE:
+                load_half_piece(k - LAST_PIECE)
+                return
             name, j = pieces[k]
             if j == 0:
                 for quadrant in range(4):
@@ -164,7 +181,9 @@ def tile_mamba2backbone_pb_kernel(
                     for g in range(GROUPS):
                         nc.tensor.matmul_mx(
                             out=bank[:, i, :],
-                            lhsT=piece[:, g, local : local + P].bitcast(FP8X4),
+                            lhsT=(
+                                piece[h][:, g, i * P : (i + 1) * P] if k == LAST_PIECE else piece[:, g, local : local + P]
+                            ).bitcast(FP8X4),
                             lhsT_scale=w_planes[4 * g : P, weight_index[name], channel : channel + P],
                             rhs=x_codes[:, g, :].bitcast(FP8X4),
                             rhs_scale=x_planes[:, g, :],
@@ -172,7 +191,7 @@ def tile_mamba2backbone_pb_kernel(
                             stop=(g == GROUPS - 1),
                         )
                 banks.append(bank)
-            if k + WEIGHT_BUFS < len(pieces):
+            if k + WEIGHT_BUFS < LOADS:
                 load_piece(k + WEIGHT_BUFS)
             return banks
 
@@ -237,7 +256,10 @@ def tile_mamba2backbone_pb_kernel(
         for rows, rows_t in ((x_rows, x_t), (deter_rows, deter_t)):
             for pair in range(CH_TILES // HALF_TILES):
                 flipped = transpose_rows(rows, pair)
-                nc.scalar.copy(out=rows_t[:, pair * HALF_TILES : (pair + 1) * HALF_TILES, :], in_=flipped[:])
+                if pair % 2 == 0:
+                    nc.scalar.copy(out=rows_t[:, pair * HALF_TILES : (pair + 1) * HALF_TILES, :], in_=flipped[:])
+                else:
+                    nc.vector.tensor_copy(out=rows_t[:, pair * HALF_TILES : (pair + 1) * HALF_TILES, :], in_=flipped[:])
 
         dt_banks, b_banks, c_banks, z_banks, back_banks = {}, {}, {}, {}, {}
         soft, decay, chain, gate = {}, {}, {}, {}

@@ -24,11 +24,13 @@ BLOCKS = CH_TILES // BLOCK_TILES
 BLOCK_CH = BLOCK_TILES * P
 HALF_TILES = 2
 HALVES = BLOCK_TILES // HALF_TILES
+LOG_STAYS = ((0,), (1,), (2, 3))
+SCALAR_EMPTIES = (1, 2, 3)
 WORDS_PER_GROUP = P * PACK // 2
 
 WEIGHT_BUFS = 12
-DT_BANKS = 2
-ACC_BANKS = 6
+DT_BANKS = 4
+ACC_BANKS = 4
 
 DT_MIN = 1e-4
 EPS = 1e-4
@@ -66,20 +68,17 @@ def tile_mamba2backbone_pb_kernel(
     weight_scales = {"dt": dt_w_scales, "b": b_w_scales, "c": c_w_scales, "z": z_w_scales}
     weight_index = {"dt": 0, "b": 1, "c": 2, "z": 3}
 
-    pieces = [("dt", 0)]
-    for j in range(BLOCKS):
-        pieces.append(("b", j))
-        if j + 1 < BLOCKS:
-            pieces.append(("dt", j + 1))
-        pieces.append(("c", j))
-        pieces.append(("z", j))
+    pieces = [("dt", 0), ("b", 0), ("dt", 1), ("c", 0), ("z", 0), ("dt", 2), ("b", 1), ("dt", 3), ("c", 1), ("z", 1)]
+    for j in (2, 3):
+        for name in ("b", "c", "z"):
+            pieces.append((name, j))
 
     with ExitStack() as stack:
         stack.enter_context(tc.manual_schedule())
         keep = stack.enter_context(tc.tile_pool(name="keep", bufs=1))
         weights = stack.enter_context(tc.tile_pool(name="weights", bufs=WEIGHT_BUFS))
         work = stack.enter_context(tc.tile_pool(name="work", bufs=2))
-        psum = stack.enter_context(tc.psum_pool(name="psum", bufs=ACC_BANKS))
+        psum = stack.enter_context(tc.psum_pool(name="psum", bufs=2))
 
         ident_bf16 = keep.tile([P, P], BF16)
         ident_f32 = keep.tile([P, P], F32)
@@ -90,6 +89,12 @@ def tile_mamba2backbone_pb_kernel(
         a_neg = keep.tile([P, CH_TILES], F32)
         a_dt_min = keep.tile([P, CH_TILES], F32)
         one = keep.tile([P, 1], F32)
+        neg_ident = keep.tile([P, P], BF16)
+        skip_cols = keep.tile([P, CH_TILES], F32)
+        skip_diag = keep.tile([P, 4, P], BF16)
+        two_ident = keep.tile([P, P], BF16)
+        first_sums = keep.tile([P, TOKEN_TILES], F32)
+        two_ident = keep.tile([P, P], BF16)
         minus_half = keep.tile([P, TOKEN_TILES], F32)
         x_rows = keep.tile([P, TOKEN_TILES, CHANNELS], BF16)
         deter_rows = keep.tile([P, TOKEN_TILES, CHANNELS], BF16)
@@ -99,7 +104,7 @@ def tile_mamba2backbone_pb_kernel(
         w_planes = keep.tile([P, len(weight_index), CHANNELS], U8, align_bytes=64)
         x_t = keep.tile([P, CH_TILES, TOKENS], BF16)
         deter_t = keep.tile([P, CH_TILES, TOKENS], BF16)
-        skip_x = keep.tile([P, CH_TILES, TOKENS], F32)
+        skip_x = keep.tile([P, 12, TOKENS], F32)
         blended = keep.tile([P, TOKEN_TILES, CHANNELS], F32)
         norm_w_all = keep.tile([P, CHANNELS], BF16)
         squares = keep.tile([P, TOKEN_TILES, BLOCKS], F32)
@@ -122,6 +127,7 @@ def tile_mamba2backbone_pb_kernel(
 
         piece_tiles = {}
 
+        LAST = BLOCKS - 1
         LAST_PIECE = len(pieces) - 1
         LOADS = LAST_PIECE + HALVES
         piece_tiles[LAST_PIECE] = []
@@ -157,24 +163,24 @@ def tile_mamba2backbone_pb_kernel(
 
         for t in range(TOKEN_TILES):
             nc.sync.dma_start(out=x_rows[:, t, :], in_=x[t * P : (t + 1) * P, :])
+        load_piece(0)
         for t in range(TOKEN_TILES):
             nc.sync.dma_start(out=deter_rows[:, t, :], in_=deter[t * P : (t + 1) * P, :])
-        for k in range(WEIGHT_BUFS):
+        for k in range(1, WEIGHT_BUFS):
             load_piece(k)
 
         make_identity(nc, ident_bf16[:])
         make_identity(nc, ident_f32[:])
         nc.gpsimd.memset(minus_half[:], -0.5)
+        nc.vector.tensor_scalar_mul(out=two_ident[:], in0=ident_bf16[:], scalar1=2.0)
+        nc.vector.tensor_scalar_mul(out=neg_ident[:], in0=ident_bf16[:], scalar1=-1.0)
 
-        def multiply(name, j):
+        def multiply(name, j, tag):
             k = pieces.index((name, j))
             piece = piece_tiles[k]
             banks = []
             for h in range(HALVES):
-                if name == "dt":
-                    bank = psum.tile([P, HALF_TILES, TOKENS], F32, tag="dt", bufs=DT_BANKS, name="dt_bank")
-                else:
-                    bank = psum.tile([P, HALF_TILES, TOKENS], F32, tag="acc", name="bank")
+                bank = psum.tile([P, HALF_TILES, TOKENS], F32, tag=tag, name="bank")
                 for i in range(HALF_TILES):
                     local = (h * HALF_TILES + i) * P
                     channel = j * BLOCK_CH + local
@@ -212,7 +218,7 @@ def tile_mamba2backbone_pb_kernel(
                 out=x_codes[:, g, :].bitcast(FP8X4), scales=x_planes[:, g, :], in_=x_grouped[:, g, :]
             )
 
-        pairs = [psum.tile([P, 2, TOKENS], F32, tag="acc", name="pairs") for g in range(GROUPS)]
+        pairs = [psum.tile([P, 2, TOKENS], F32, tag="AABB"[g], name="pairs") for g in range(GROUPS)]
         for t in range(TOKEN_TILES):
             for g in range(GROUPS):
                 for u in range(2):
@@ -223,16 +229,20 @@ def tile_mamba2backbone_pb_kernel(
                         ],
                         ident_f32[:],
                     )
-        for g in range(GROUPS):
-            nc.vector.tensor_copy(
+        def group_words(g, copy):
+            copy(
                 out=x_grouped[:, g, :].bitcast(F32).rearrange("p (r u) -> p r u", u=2),
                 in_=pairs[g][:].rearrange("p u r -> p r u"),
             )
-            if g > 0:
-                quantise(g - 1)
-        quantise(GROUPS - 1)
 
-        vector_cols = psum.tile([P, P], BF16, tag="acc", name="vector_cols")
+        group_words(0, nc.vector.tensor_copy)
+        group_words(1, nc.scalar.copy)
+        group_words(2, nc.vector.tensor_copy)
+        group_words(3, nc.scalar.copy)
+        for g in range(GROUPS):
+            quantise(g)
+
+        vector_cols = psum.tile([P, P], BF16, tag="C", name="vector_cols")
         nc.tensor.transpose(vector_cols[:], vector_rows[:], ident_bf16[:])
         nc.scalar.copy(out=per_channel[:], in_=vector_cols[:])
         a_base_cols = per_channel[:, CH_TILES * A_BASE : CH_TILES * (A_BASE + 1)]
@@ -242,9 +252,19 @@ def tile_mamba2backbone_pb_kernel(
             out=half_z_b[:], in0=per_channel[:, CH_TILES * Z_B : CH_TILES * (Z_B + 1)], scalar1=0.5
         )
         nc.vector.tensor_scalar_min(out=soft_a[:], in0=soft_a[:], scalar1=LN_MAX)
+        nc.vector.tensor_copy(out=skip_cols[:], in_=per_channel[:, CH_TILES * SKIP : CH_TILES * (SKIP + 1)])
+        for i in range(4):
+            nc.gpsimd.tensor_scalar(
+                out=skip_diag[:, i, :],
+                in0=ident_bf16[:],
+                scalar1=skip_cols[:, 12 + i : 12 + i + 1],
+                scalar2=0.0,
+                op0=ALU.mult,
+                op1=ALU.add,
+            )
 
         def transpose_rows(rows, pair):
-            flipped = psum.tile([P, HALF_TILES, TOKENS], BF16, tag="acc", name="flipped")
+            flipped = psum.tile([P, HALF_TILES, TOKENS], BF16, tag=FLIP_TAGS[rows is deter_rows][pair], name="flipped")
             for i in range(HALF_TILES):
                 ct = pair * HALF_TILES + i
                 for t in range(TOKEN_TILES):
@@ -253,19 +273,23 @@ def tile_mamba2backbone_pb_kernel(
                     )
             return flipped
 
-        for rows, rows_t in ((x_rows, x_t), (deter_rows, deter_t)):
-            for pair in range(CH_TILES // HALF_TILES):
+        FLIP_TAGS = ("CCDDAABB", "DDAABBDA")
+
+        def flip(rows, rows_t, pairs_of_tiles):
+            for pair in pairs_of_tiles:
                 flipped = transpose_rows(rows, pair)
-                if pair % 2 == 0:
+                if pair % 2 == 0 and rows is x_rows:
                     nc.scalar.copy(out=rows_t[:, pair * HALF_TILES : (pair + 1) * HALF_TILES, :], in_=flipped[:])
                 else:
                     nc.vector.tensor_copy(out=rows_t[:, pair * HALF_TILES : (pair + 1) * HALF_TILES, :], in_=flipped[:])
+
+        flip(x_rows, x_t, range(CH_TILES // HALF_TILES))
 
         dt_banks, b_banks, c_banks, z_banks, back_banks = {}, {}, {}, {}, {}
         soft, decay, chain, gate = {}, {}, {}, {}
 
         def softplus_exp(j):
-            soft[j] = work.tile([P, BLOCK_TILES, TOKENS], F32, tag="soft", name="soft")
+            soft[j] = work.tile([P, BLOCK_TILES, TOKENS], F32, tag="soft", bufs=BLOCKS, name="soft")
             for i, h, ih, ct in tiles_of(j):
                 nc.scalar.activation(
                     out=soft[j][:, i, :], in_=dt_banks[j][h][:, ih, :], func=ACT.Exp, bias=channel_scalar(DT_B, ct)
@@ -311,6 +335,20 @@ def tile_mamba2backbone_pb_kernel(
                     op0=ALU.mult,
                     op1=ALU.subtract,
                 )
+
+        skip_banks = {}
+
+        def skip_product(j):
+            skip_banks[j] = []
+            for h in range(HALVES):
+                bank = psum.tile([P, HALF_TILES, TOKENS], F32, tag="A", name="skip_bank")
+                for ih in range(HALF_TILES):
+                    ct = j * BLOCK_TILES + h * HALF_TILES + ih
+                    nc.tensor.matmul(
+                        bank[:, ih, :], lhsT=skip_diag[:, ct - 12, :], rhs=x_t[:, ct, :], start=True, stop=False
+                    )
+                    nc.tensor.matmul(bank[:, ih, :], lhsT=neg_ident[:], rhs=deter_t[:, ct, :], start=False, stop=True)
+                skip_banks[j].append(bank)
 
         def tanh_b(j):
             chain[j] = work.tile([P, BLOCK_TILES, TOKENS], F32, tag="chain", name="chain")
@@ -371,128 +409,231 @@ def tile_mamba2backbone_pb_kernel(
                 )
 
         def plus_skip_term(j):
-            for mine, whole in half_slices(j):
+            for h, (mine, whole) in enumerate(half_slices(j)):
                 nc.vector.tensor_tensor(
-                    out=chain[j][:, mine, :], in0=chain[j][:, mine, :], in1=skip_x[:, whole, :], op=ALU.add
+                    out=chain[j][:, mine, :],
+                    in0=chain[j][:, mine, :],
+                    in1=skip_banks[j][h][:] if j in skip_banks else skip_x[:, whole, :],
+                    op=ALU.add,
                 )
 
         def times_gate(j):
-            for mine, whole in half_slices(j):
+            if j == LAST:
+                parts = [(slice(0, BLOCK_TILES), slice(t * P, (t + 1) * P)) for t in range(TOKEN_TILES)]
+            else:
+                parts = [(mine, slice(0, TOKENS)) for mine, whole in half_slices(j)]
+            for tiles, tokens in parts:
                 nc.vector.scalar_tensor_tensor(
-                    out=chain[j][:, mine, :],
-                    in0=gate[j][:, mine, :],
+                    out=chain[j][:, tiles, tokens],
+                    in0=gate[j][:, tiles, tokens],
                     scalar=1.0,
-                    in1=chain[j][:, mine, :],
+                    in1=chain[j][:, tiles, tokens],
                     op0=ALU.add,
                     op1=ALU.mult,
                 )
 
-        def transpose_back(j):
+        def transpose_back(j, tag):
             back_banks[j] = []
             for t in range(TOKEN_TILES):
-                back = psum.tile([P, BLOCK_CH], F32, tag="acc", name="back")
-                for i in range(BLOCK_TILES):
-                    nc.tensor.transpose(
-                        back[:, i * P : (i + 1) * P], chain[j][:, i, t * P : (t + 1) * P], ident_f32[:]
+                back = psum.tile([P, BLOCK_CH], F32, tag=tag, name="back")
+                if j in SCALAR_EMPTIES:
+                    nc.tensor.matmul(
+                        back[:],
+                        lhsT=two_ident[:],
+                        rhs=deter_rows[:, t, j * BLOCK_CH : (j + 1) * BLOCK_CH],
+                        start=True,
+                        stop=False,
                     )
+                for i in range(BLOCK_TILES):
+                    part = back[:, i * P : (i + 1) * P]
+                    turned = chain[j][:, i, t * P : (t + 1) * P]
+                    if j in SCALAR_EMPTIES:
+                        nc.tensor.matmul(
+                            part,
+                            lhsT=turned,
+                            rhs=ident_f32[:],
+                            is_transpose=True,
+                            start=False,
+                            stop=(i == BLOCK_TILES - 1),
+                        )
+                    else:
+                        nc.tensor.transpose(part, turned, ident_f32[:])
                 back_banks[j].append(back)
+
+        def block_columns(j, t):
+            return blended[:, t, j * BLOCK_CH : (j + 1) * BLOCK_CH]
 
         def blend(j):
             for t in range(TOKEN_TILES):
-                nc.vector.scalar_tensor_tensor(
-                    out=blended[:, t, j * BLOCK_CH : (j + 1) * BLOCK_CH],
-                    in0=back_banks[j][t][:],
-                    scalar=0.5,
-                    in1=deter_rows[:, t, j * BLOCK_CH : (j + 1) * BLOCK_CH],
-                    op0=ALU.mult,
-                    op1=ALU.add,
-                )
+                if j in SCALAR_EMPTIES:
+                    nc.scalar.activation(out=block_columns(j, t), in_=back_banks[j][t][:], func=ACT.Copy, scale=0.5)
+                else:
+                    nc.vector.scalar_tensor_tensor(
+                        out=block_columns(j, t),
+                        in0=back_banks[j][t][:],
+                        scalar=0.5,
+                        in1=deter_rows[:, t, j * BLOCK_CH : (j + 1) * BLOCK_CH],
+                        op0=ALU.mult,
+                        op1=ALU.add,
+                    )
 
         def sum_squares(j):
             for t in range(TOKEN_TILES):
                 unread = work.tile([P, BLOCK_CH], F32, tag="unread", name="unread")
                 nc.scalar.activation(
-                    out=unread[:],
-                    in_=blended[:, t, j * BLOCK_CH : (j + 1) * BLOCK_CH],
-                    func=ACT.Square,
-                    accum_out=squares[:, t, j : j + 1],
+                    out=unread[:], in_=block_columns(j, t), func=ACT.Square, accum_out=squares[:, t, j : j + 1]
                 )
 
-        dt_banks[0] = multiply("dt", 0)
+        def product(name, j):
+            tag = TAGS[name + str(j)]
+            {"dt": dt_banks, "b": b_banks, "c": c_banks, "z": z_banks}[name][j] = multiply(name, j, tag)
+
+        TAGS = dict(b0="A", dt0="C", dt1="D", c0="B", z0="A", dt2="C", b1="B", dt3="D", T0="A", c1="B", z1="A", b2="B", c2="C", T1="A", z2="D", b3="B", c3="C", T2="A", z3="D", T3="B")
+        def TB(j): transpose_back(j, TAGS["T" + str(j)])
+
+        product("dt", 0)
         softplus_exp(0)
-        for j in range(BLOCKS - 1):
-            skip_term(j)
+        flip(deter_rows, deter_t, range(8))
         softplus_cut(0)
-        skip_term(BLOCKS - 1)
+        skip_term(0)
         nc.scalar.activation(out=soft_a[:], in_=soft_a[:], func=ACT.Ln, bias=one[:])
         softplus_log(0)
         nc.vector.tensor_tensor(out=soft_a[:], in0=soft_a[:], in1=a_base_cols, op=ALU.max)
         nc.vector.tensor_scalar_mul(out=a_neg[:], in0=soft_a[:], scalar1=-1.0)
         nc.vector.tensor_scalar_mul(out=a_dt_min[:], in0=soft_a[:], scalar1=-DT_MIN)
         softplus_max(0)
+        skip_term(1)
+        skip_term(2)
         decay_exp(0)
-        b_banks[0] = multiply("b", 0)
-        dt_banks[1] = multiply("dt", 1)
+        product("b", 0)
+        product("dt", 1)
 
-        for j in range(BLOCKS):
-            more = j + 1 < BLOCKS
-            c_banks[j] = multiply("c", j)
-            tanh_b(j)
-            z_banks[j] = multiply("z", j)
-            if j == 1:
-                nc.sync.dma_start(out=norm_w_all[:], in_=norm_w.partition_broadcast(P))
-            decay_times_deter(j)
-            if j > 0:
-                blend(j - 1)
-            b_times_x(j)
-            if more:
-                softplus_exp(j + 1)
-                softplus_cut(j + 1)
-            if j > 0:
-                sum_squares(j - 1)
-            if more:
-                softplus_log(j + 1)
-            times_dt(j)
-            new_state(j)
-            times_c(j)
-            if more:
-                softplus_max(j + 1)
-            tanh_z(j)
-            if more:
-                decay_exp(j + 1)
-            plus_skip_term(j)
-            times_gate(j)
-            if more:
-                b_banks[j + 1] = multiply("b", j + 1)
-            if j + 2 < BLOCKS:
-                dt_banks[j + 2] = multiply("dt", j + 2)
-            transpose_back(j)
-        blend(BLOCKS - 1)
-        sum_squares(BLOCKS - 1)
+        product("c", 0)
+        tanh_b(0)
+        decay_times_deter(0)
+        product("z", 0)
+        softplus_exp(1)
+        b_times_x(0)
+        softplus_cut(1)
+        softplus_log(1)
+        times_dt(0)
+        new_state(0)
+        times_c(0)
+        product("dt", 2)
+        softplus_max(1)
+        tanh_z(0)
+        decay_exp(1)
+        softplus_exp(2)
+        plus_skip_term(0)
+        times_gate(0)
+        softplus_cut(2)
+        product("b", 1)
+        product("dt", 3)
+        TB(0)
 
-        for t in range(TOKEN_TILES):
-            mine = slice(t, t + 1)
-            nc.vector.tensor_reduce(
-                out=mean_sq[:, mine], in_=squares[:, t, :], axis=mybir.AxisListType.X, op=ALU.add
+        product("c", 1)
+        tanh_b(1)
+        decay_times_deter(1)
+        softplus_exp(3)
+        b_times_x(1)
+        blend(0)
+        product("z", 1)
+        softplus_cut(3)
+        softplus_log(2)
+        softplus_log(3)
+        sum_squares(0)
+        times_dt(1)
+        new_state(1)
+        times_c(1)
+        softplus_max(2)
+        tanh_z(1)
+        decay_exp(2)
+        plus_skip_term(1)
+        times_gate(1)
+        softplus_max(3)
+        product("b", 2)
+        product("c", 2)
+        TB(1)
+
+        tanh_b(2)
+        decay_times_deter(2)
+        product("z", 2)
+        b_times_x(2)
+        product("b", 3)
+        times_dt(2)
+        new_state(2)
+        times_c(2)
+        decay_exp(3)
+        blend(1)
+        sum_squares(1)
+        product("c", 3)
+        tanh_z(2)
+        plus_skip_term(2)
+        times_gate(2)
+        TB(2)
+
+        tanh_b(3)
+        decay_times_deter(3)
+        product("z", 3)
+        nc.sync.dma_start(out=norm_w_all[:], in_=norm_w.partition_broadcast(P))
+        b_times_x(3)
+        times_dt(3)
+        new_state(3)
+        blend(2)
+        sum_squares(2)
+        times_c(3)
+        nc.vector.tensor_reduce(out=first_sums[:], in_=squares[:, :, :LAST], axis=mybir.AxisListType.X, op=ALU.add)
+        skip_product(3)
+        tanh_z(3)
+        plus_skip_term(3)
+        nc.vector.tensor_scalar(
+            out=first_sums[:], in0=first_sums[:], scalar1=1.0 / CHANNELS, scalar2=EPS, op0=ALU.mult, op1=ALU.add
+        )
+        times_gate(3)
+        TB(3)
+
+        def last_columns(t):
+            return blended[:, t, LAST * BLOCK_CH : CHANNELS]
+
+        def square_last(t):
+            unread = work.tile([P, BLOCK_CH], F32, tag="unread", name="unread")
+            nc.scalar.activation(
+                out=unread[:], in_=back_banks[LAST][t][:], func=ACT.Square, scale=0.5, accum_out=squares[:, t, LAST : LAST + 1]
             )
-            nc.vector.tensor_scalar(
+
+        def factor(t):
+            mine = slice(t, t + 1)
+            nc.vector.scalar_tensor_tensor(
                 out=mean_sq[:, mine],
-                in0=mean_sq[:, mine],
-                scalar1=1.0 / CHANNELS,
-                scalar2=EPS,
+                in0=squares[:, t, LAST : LAST + 1],
+                scalar=1.0 / CHANNELS,
+                in1=first_sums[:, mine],
                 op0=ALU.mult,
                 op1=ALU.add,
             )
             nc.gpsimd.tensor_tensor(out=rstd[:, mine], in0=mean_sq[:, mine], in1=minus_half[:, mine], op=ALU.pow)
-        for t in range(TOKEN_TILES):
-            for j in range(BLOCKS):
-                columns = slice(j * BLOCK_CH, (j + 1) * BLOCK_CH)
-                nc.vector.scalar_tensor_tensor(
-                    out=blended[:, t, columns],
-                    in0=blended[:, t, columns],
-                    scalar=rstd[:, t : t + 1],
-                    in1=norm_w_all[:, columns],
-                    op0=ALU.mult,
-                    op1=ALU.mult,
-                )
-                nc.sync.dma_start(out=out[t * P : (t + 1) * P, columns], in_=blended[:, t, columns])
+
+
+        def scale_and_store(t, j):
+            columns = slice(j * BLOCK_CH, (j + 1) * BLOCK_CH)
+            nc.vector.scalar_tensor_tensor(
+                out=blended[:, t, columns],
+                in0=blended[:, t, columns],
+                scalar=rstd[:, t : t + 1],
+                in1=norm_w_all[:, columns],
+                op0=ALU.mult,
+                op1=ALU.mult,
+            )
+            nc.sync.dma_start(out=out[t * P : (t + 1) * P, columns], in_=blended[:, t, columns])
+
+        square_last(0)
+        factor(0)
+        nc.vector.tensor_scalar_mul(out=last_columns(0), in0=back_banks[LAST][0][:], scalar1=0.5)
+        square_last(1)
+        nc.scalar.activation(out=last_columns(1), in_=back_banks[LAST][1][:], func=ACT.Copy, scale=0.5)
+        scale_and_store(0, 0)
+        factor(1)
+        for j in range(1, BLOCKS):
+            scale_and_store(0, j)
+        for j in range(BLOCKS):
+            scale_and_store(1, j)

@@ -124,6 +124,7 @@ def tile_mamba2backbone_pb_kernel(
 
         nc.vector.memset(w_planes[:].bitcast(I32), 0)
         nc.vector.memset(one[:], 1.0)
+        nc.scalar.activation(out=rstd[:, 0:1], in_=one[:], func=ACT.Exp)
 
         piece_tiles = {}
 
@@ -149,9 +150,9 @@ def tile_mamba2backbone_pb_kernel(
             name, j = pieces[k]
             if j == 0:
                 for quadrant in range(4):
-                    nc.sync.dma_start(
-                        out=w_planes[32 * quadrant : 32 * quadrant + 16, weight_index[name], :].bitcast(I32),
-                        in_=weight_scales[name][:, 4 * quadrant : 4 * quadrant + 4, :].bitcast(I32),
+                    nc.gpsimd.dma_start(
+                        out=w_planes[32 * quadrant : 32 * quadrant + 16, weight_index[name], :].bitcast(F32),
+                        in_=weight_scales[name][:, 4 * quadrant : 4 * quadrant + 4, :].bitcast(F32),
                     )
             piece = weights.tile([P, GROUPS, BLOCK_CH], U32, align_bytes=64, tag="piece", name="piece")
             by_partition = weight_words[name].rearrange("g p n t -> p g (n t)")
@@ -161,6 +162,9 @@ def tile_mamba2backbone_pb_kernel(
             )
             piece_tiles[k] = piece
 
+        make_identity(nc, ident_f32[:])
+        make_identity(nc, ident_bf16[:])
+        nc.gpsimd.memset(minus_half[:], -0.5)
         for t in range(TOKEN_TILES):
             nc.sync.dma_start(out=x_rows[:, t, :], in_=x[t * P : (t + 1) * P, :])
         load_piece(0)
@@ -169,9 +173,6 @@ def tile_mamba2backbone_pb_kernel(
         for k in range(1, WEIGHT_BUFS):
             load_piece(k)
 
-        make_identity(nc, ident_bf16[:])
-        make_identity(nc, ident_f32[:])
-        nc.gpsimd.memset(minus_half[:], -0.5)
         nc.vector.tensor_scalar_mul(out=two_ident[:], in0=ident_bf16[:], scalar1=2.0)
         nc.vector.tensor_scalar_mul(out=neg_ident[:], in0=ident_bf16[:], scalar1=-1.0)
 
@@ -273,7 +274,7 @@ def tile_mamba2backbone_pb_kernel(
                     )
             return flipped
 
-        FLIP_TAGS = ("CCDDAABB", "DDAABBDA")
+        FLIP_TAGS = ("DDAABBDD", "AABBAABB")
 
         def flip(rows, rows_t, pairs_of_tiles):
             for pair in pairs_of_tiles:
@@ -295,8 +296,8 @@ def tile_mamba2backbone_pb_kernel(
                     out=soft[j][:, i, :], in_=dt_banks[j][h][:, ih, :], func=ACT.Exp, bias=channel_scalar(DT_B, ct)
                 )
 
-        def softplus_cut(j):
-            for mine, whole in half_slices(j):
+        def softplus_cut(j, halves=slice(0, HALVES)):
+            for mine, whole in half_slices(j)[halves]:
                 nc.vector.tensor_scalar_min(out=soft[j][:, mine, :], in0=soft[j][:, mine, :], scalar1=LN_MAX)
 
         def softplus_log(j):
@@ -493,8 +494,10 @@ def tile_mamba2backbone_pb_kernel(
 
         product("dt", 0)
         softplus_exp(0)
-        flip(deter_rows, deter_t, range(8))
-        softplus_cut(0)
+        softplus_cut(0, slice(0, 1))
+        flip(deter_rows, deter_t, range(2))
+        softplus_cut(0, slice(1, 2))
+        flip(deter_rows, deter_t, range(2, 8))
         skip_term(0)
         nc.scalar.activation(out=soft_a[:], in_=soft_a[:], func=ACT.Ln, bias=one[:])
         softplus_log(0)
@@ -541,13 +544,13 @@ def tile_mamba2backbone_pb_kernel(
         softplus_cut(3)
         softplus_log(2)
         softplus_log(3)
-        sum_squares(0)
         times_dt(1)
         new_state(1)
         times_c(1)
         softplus_max(2)
         tanh_z(1)
         decay_exp(2)
+        sum_squares(0)
         plus_skip_term(1)
         times_gate(1)
         softplus_max(3)

@@ -150,9 +150,10 @@ def tile_mamba2backbone_pb_kernel(
             name, j = pieces[k]
             if j == 0:
                 for quadrant in range(4):
-                    nc.gpsimd.dma_start(
-                        out=w_planes[32 * quadrant : 32 * quadrant + 16, weight_index[name], :].bitcast(F32),
-                        in_=weight_scales[name][:, 4 * quadrant : 4 * quadrant + 4, :].bitcast(F32),
+                    queue, word = (nc.gpsimd, F32) if name in ("c", "z") else (nc.sync, I32)
+                    queue.dma_start(
+                        out=w_planes[32 * quadrant : 32 * quadrant + 16, weight_index[name], :].bitcast(word),
+                        in_=weight_scales[name][:, 4 * quadrant : 4 * quadrant + 4, :].bitcast(word),
                     )
             piece = weights.tile([P, GROUPS, BLOCK_CH], U32, align_bytes=64, tag="piece", name="piece")
             by_partition = weight_words[name].rearrange("g p n t -> p g (n t)")

@@ -130,31 +130,33 @@ def tile_mamba2backbone_pb_kernel(
 
         LAST = BLOCKS - 1
         LAST_PIECE = len(pieces) - 1
-        LOADS = LAST_PIECE + HALVES
-        piece_tiles[LAST_PIECE] = []
+        IN_HALVES = (0, LAST_PIECE)
+        LOADS = len(pieces)
 
-        def load_half_piece(h):
-            name, j = pieces[LAST_PIECE]
+        def load_half_piece(k, h):
+            name, j = pieces[k]
             by_partition = weight_words[name].rearrange("g p n t -> p g (n t)")
             half = weights.tile([P, GROUPS, HALF_TILES * P], U32, align_bytes=64, tag="piece", name="half_piece")
             first = PACK * (BLOCK_CH * j + HALF_TILES * P * h)
             nc.sync.dma_start(
                 out=half[:].bitcast(I32), in_=by_partition[:, :, first : first + PACK * HALF_TILES * P].bitcast(I32)
             )
-            piece_tiles[LAST_PIECE].append(half)
+            piece_tiles[k].append(half)
 
         def load_piece(k):
-            if k >= LAST_PIECE:
-                load_half_piece(k - LAST_PIECE)
-                return
             name, j = pieces[k]
             if j == 0:
                 for quadrant in range(4):
-                    queue, word = (nc.gpsimd, F32) if name in ("c", "z") else (nc.sync, I32)
+                    queue, word = (nc.gpsimd, F32) if name in ("b", "c", "z") else (nc.sync, I32)
                     queue.dma_start(
                         out=w_planes[32 * quadrant : 32 * quadrant + 16, weight_index[name], :].bitcast(word),
                         in_=weight_scales[name][:, 4 * quadrant : 4 * quadrant + 4, :].bitcast(word),
                     )
+            if k in IN_HALVES:
+                piece_tiles[k] = []
+                for h in range(HALVES):
+                    load_half_piece(k, h)
+                return
             piece = weights.tile([P, GROUPS, BLOCK_CH], U32, align_bytes=64, tag="piece", name="piece")
             by_partition = weight_words[name].rearrange("g p n t -> p g (n t)")
             nc.sync.dma_start(
@@ -190,7 +192,7 @@ def tile_mamba2backbone_pb_kernel(
                         nc.tensor.matmul_mx(
                             out=bank[:, i, :],
                             lhsT=(
-                                piece[h][:, g, i * P : (i + 1) * P] if k == LAST_PIECE else piece[:, g, local : local + P]
+                                piece[h][:, g, i * P : (i + 1) * P] if k in IN_HALVES else piece[:, g, local : local + P]
                             ).bitcast(FP8X4),
                             lhsT_scale=w_planes[4 * g : P, weight_index[name], channel : channel + P],
                             rhs=x_codes[:, g, :].bitcast(FP8X4),
@@ -343,7 +345,7 @@ def tile_mamba2backbone_pb_kernel(
         def skip_product(j):
             skip_banks[j] = []
             for h in range(HALVES):
-                bank = psum.tile([P, HALF_TILES, TOKENS], F32, tag="A", name="skip_bank")
+                bank = psum.tile([P, HALF_TILES, TOKENS], F32, tag="B", name="skip_bank")
                 for ih in range(HALF_TILES):
                     ct = j * BLOCK_TILES + h * HALF_TILES + ih
                     nc.tensor.matmul(
@@ -411,13 +413,15 @@ def tile_mamba2backbone_pb_kernel(
                 )
 
         def plus_skip_term(j):
-            for h, (mine, whole) in enumerate(half_slices(j)):
-                nc.vector.tensor_tensor(
-                    out=chain[j][:, mine, :],
-                    in0=chain[j][:, mine, :],
-                    in1=skip_banks[j][h][:] if j in skip_banks else skip_x[:, whole, :],
-                    op=ALU.add,
-                )
+            parts = [slice(t * P, (t + 1) * P) for t in range(TOKEN_TILES)] if j == LAST else [slice(0, TOKENS)]
+            for tokens in parts:
+                for h, (mine, whole) in enumerate(half_slices(j)):
+                    nc.vector.tensor_tensor(
+                        out=chain[j][:, mine, tokens],
+                        in0=chain[j][:, mine, tokens],
+                        in1=(skip_banks[j][h][:] if j in skip_banks else skip_x[:, whole, :])[:, :, tokens],
+                        op=ALU.add,
+                    )
 
         def times_gate(j):
             if j == LAST:
@@ -490,7 +494,7 @@ def tile_mamba2backbone_pb_kernel(
             tag = TAGS[name + str(j)]
             {"dt": dt_banks, "b": b_banks, "c": c_banks, "z": z_banks}[name][j] = multiply(name, j, tag)
 
-        TAGS = dict(b0="A", dt0="C", dt1="D", c0="B", z0="A", dt2="C", b1="B", dt3="D", T0="A", c1="B", z1="A", b2="B", c2="C", T1="A", z2="D", b3="B", c3="C", T2="A", z3="D", T3="B")
+        TAGS = dict(b0="A", dt0="C", dt1="D", c0="B", z0="A", dt2="C", b1="B", dt3="D", T0="A", c1="B", z1="A", b2="B", c2="C", T1="A", z2="D", b3="B", c3="C", T2="A", z3="D", T3="C")
         def TB(j): transpose_back(j, TAGS["T" + str(j)])
 
         product("dt", 0)
@@ -578,6 +582,7 @@ def tile_mamba2backbone_pb_kernel(
 
         tanh_b(3)
         decay_times_deter(3)
+        skip_product(3)
         product("z", 3)
         nc.sync.dma_start(out=norm_w_all[:], in_=norm_w.partition_broadcast(P))
         b_times_x(3)
@@ -587,7 +592,6 @@ def tile_mamba2backbone_pb_kernel(
         sum_squares(2)
         times_c(3)
         nc.vector.tensor_reduce(out=first_sums[:], in_=squares[:, :, :LAST], axis=mybir.AxisListType.X, op=ALU.add)
-        skip_product(3)
         tanh_z(3)
         plus_skip_term(3)
         nc.vector.tensor_scalar(
@@ -618,8 +622,9 @@ def tile_mamba2backbone_pb_kernel(
             nc.gpsimd.tensor_tensor(out=rstd[:, mine], in0=mean_sq[:, mine], in1=minus_half[:, mine], op=ALU.pow)
 
 
-        def scale_and_store(t, j):
-            columns = slice(j * BLOCK_CH, (j + 1) * BLOCK_CH)
+        def scale_and_store(t, j, part=0, parts=1):
+            first = j * BLOCK_CH + part * BLOCK_CH // parts
+            columns = slice(first, first + BLOCK_CH // parts)
             nc.vector.scalar_tensor_tensor(
                 out=blended[:, t, columns],
                 in0=blended[:, t, columns],
@@ -635,8 +640,9 @@ def tile_mamba2backbone_pb_kernel(
         nc.vector.tensor_scalar_mul(out=last_columns(0), in0=back_banks[LAST][0][:], scalar1=0.5)
         square_last(1)
         nc.scalar.activation(out=last_columns(1), in_=back_banks[LAST][1][:], func=ACT.Copy, scale=0.5)
-        scale_and_store(0, 0)
+        scale_and_store(0, 0, 0, 2)
         factor(1)
+        scale_and_store(0, 0, 1, 2)
         for j in range(1, BLOCKS):
             scale_and_store(0, j)
         for j in range(BLOCKS):

@@ -92,10 +92,8 @@ def tile_mamba2backbone_pb_kernel(
         neg_ident = keep.tile([P, P], BF16)
         skip_cols = keep.tile([P, CH_TILES], F32)
         skip_diag = keep.tile([P, 4, P], BF16)
-        two_ident = keep.tile([P, P], BF16)
         first_sums = keep.tile([P, TOKEN_TILES], F32)
         two_ident = keep.tile([P, P], BF16)
-        minus_half = keep.tile([P, TOKEN_TILES], F32)
         x_rows = keep.tile([P, TOKEN_TILES, CHANNELS], BF16)
         deter_rows = keep.tile([P, TOKEN_TILES, CHANNELS], BF16)
         x_grouped = keep.tile([P, GROUPS, TOKENS * PACK], BF16, align_bytes=64)
@@ -167,7 +165,6 @@ def tile_mamba2backbone_pb_kernel(
 
         make_identity(nc, ident_f32[:])
         make_identity(nc, ident_bf16[:])
-        nc.gpsimd.memset(minus_half[:], -0.5)
         for t in range(TOKEN_TILES):
             nc.sync.dma_start(out=x_rows[:, t, :], in_=x[t * P : (t + 1) * P, :])
         load_piece(0)
@@ -401,46 +398,42 @@ def tile_mamba2backbone_pb_kernel(
                     out=chain[j][:, mine, :], in0=chain[j][:, mine, :], in1=decay[j][:, mine, :], op=ALU.add
                 )
 
-        def times_c(j):
+        ALL_TOKENS = slice(0, TOKENS)
+
+        def times_c(j, tokens=ALL_TOKENS):
             for i, h, ih, ct in tiles_of(j):
                 nc.vector.scalar_tensor_tensor(
-                    out=chain[j][:, i, :],
-                    in0=c_banks[j][h][:, ih, :],
+                    out=chain[j][:, i, tokens],
+                    in0=c_banks[j][h][:, ih, tokens],
                     scalar=channel_scalar(C_B, ct),
-                    in1=chain[j][:, i, :],
+                    in1=chain[j][:, i, tokens],
                     op0=ALU.add,
                     op1=ALU.mult,
                 )
 
-        def plus_skip_term(j):
-            parts = [slice(t * P, (t + 1) * P) for t in range(TOKEN_TILES)] if j == LAST else [slice(0, TOKENS)]
-            for tokens in parts:
-                for h, (mine, whole) in enumerate(half_slices(j)):
-                    nc.vector.tensor_tensor(
-                        out=chain[j][:, mine, tokens],
-                        in0=chain[j][:, mine, tokens],
-                        in1=(skip_banks[j][h][:] if j in skip_banks else skip_x[:, whole, :])[:, :, tokens],
-                        op=ALU.add,
-                    )
+        def plus_skip_term(j, tokens=ALL_TOKENS):
+            for h, (mine, whole) in enumerate(half_slices(j)):
+                nc.vector.tensor_tensor(
+                    out=chain[j][:, mine, tokens],
+                    in0=chain[j][:, mine, tokens],
+                    in1=(skip_banks[j][h][:] if j in skip_banks else skip_x[:, whole, :])[:, :, tokens],
+                    op=ALU.add,
+                )
 
-        def times_gate(j):
-            if j == LAST:
-                parts = [(slice(0, BLOCK_TILES), slice(t * P, (t + 1) * P)) for t in range(TOKEN_TILES)]
-            else:
-                parts = [(mine, slice(0, TOKENS)) for mine, whole in half_slices(j)]
-            for tiles, tokens in parts:
+        def times_gate(j, tokens=ALL_TOKENS):
+            for mine, whole in half_slices(j):
                 nc.vector.scalar_tensor_tensor(
-                    out=chain[j][:, tiles, tokens],
-                    in0=gate[j][:, tiles, tokens],
+                    out=chain[j][:, mine, tokens],
+                    in0=gate[j][:, mine, tokens],
                     scalar=1.0,
-                    in1=chain[j][:, tiles, tokens],
+                    in1=chain[j][:, mine, tokens],
                     op0=ALU.add,
                     op1=ALU.mult,
                 )
 
-        def transpose_back(j, tag):
-            back_banks[j] = []
-            for t in range(TOKEN_TILES):
+        def transpose_back(j, tag, token_tiles=range(TOKEN_TILES)):
+            back_banks.setdefault(j, [])
+            for t in token_tiles:
                 back = psum.tile([P, BLOCK_CH], F32, tag=tag, name="back")
                 if j in SCALAR_EMPTIES:
                     nc.tensor.matmul(
@@ -489,6 +482,43 @@ def tile_mamba2backbone_pb_kernel(
                 nc.scalar.activation(
                     out=unread[:], in_=block_columns(j, t), func=ACT.Square, accum_out=squares[:, t, j : j + 1]
                 )
+
+        def last_columns(t):
+            return blended[:, t, LAST * BLOCK_CH : CHANNELS]
+
+        def square_last(t):
+            unread = work.tile([P, BLOCK_CH], F32, tag="unread", name="unread")
+            nc.scalar.activation(
+                out=unread[:], in_=back_banks[LAST][t][:], func=ACT.Square, scale=0.5, accum_out=squares[:, t, LAST : LAST + 1]
+            )
+
+        def root(t):
+            nc.scalar.activation(
+                out=mean_sq[:, t : t + 1],
+                in_=squares[:, t, LAST : LAST + 1],
+                func=ACT.Sqrt,
+                scale=1.0 / CHANNELS,
+                bias=first_sums[:, t : t + 1],
+            )
+
+        def factor(t):
+            nc.vector.reciprocal(out=rstd[:, t : t + 1], in_=mean_sq[:, t : t + 1])
+
+        def take_out(t):
+            nc.scalar.activation(out=last_columns(t), in_=back_banks[LAST][t][:], func=ACT.Copy, scale=0.5)
+
+        def scale_and_store(t, j, part=0, parts=1):
+            first = j * BLOCK_CH + part * BLOCK_CH // parts
+            columns = slice(first, first + BLOCK_CH // parts)
+            nc.vector.scalar_tensor_tensor(
+                out=blended[:, t, columns],
+                in0=blended[:, t, columns],
+                scalar=rstd[:, t : t + 1],
+                in1=norm_w_all[:, columns],
+                op0=ALU.mult,
+                op1=ALU.mult,
+            )
+            nc.sync.dma_start(out=out[t * P : (t + 1) * P, columns], in_=blended[:, t, columns])
 
         def product(name, j):
             tag = TAGS[name + str(j)]
@@ -582,68 +612,42 @@ def tile_mamba2backbone_pb_kernel(
 
         tanh_b(3)
         decay_times_deter(3)
-        skip_product(3)
         product("z", 3)
+        skip_product(3)
         nc.sync.dma_start(out=norm_w_all[:], in_=norm_w.partition_broadcast(P))
         b_times_x(3)
         times_dt(3)
         new_state(3)
         blend(2)
         sum_squares(2)
-        times_c(3)
+        first_tokens, second_tokens = (slice(t * P, (t + 1) * P) for t in range(TOKEN_TILES))
+        times_c(3, first_tokens)
         nc.vector.tensor_reduce(out=first_sums[:], in_=squares[:, :, :LAST], axis=mybir.AxisListType.X, op=ALU.add)
         tanh_z(3)
-        plus_skip_term(3)
+        nc.scalar.activation(out=mean_sq[:, 0:1], in_=one[:], func=ACT.Sqrt)
+        plus_skip_term(3, first_tokens)
         nc.vector.tensor_scalar(
             out=first_sums[:], in0=first_sums[:], scalar1=1.0 / CHANNELS, scalar2=EPS, op0=ALU.mult, op1=ALU.add
         )
-        times_gate(3)
-        TB(3)
-
-        def last_columns(t):
-            return blended[:, t, LAST * BLOCK_CH : CHANNELS]
-
-        def square_last(t):
-            unread = work.tile([P, BLOCK_CH], F32, tag="unread", name="unread")
-            nc.scalar.activation(
-                out=unread[:], in_=back_banks[LAST][t][:], func=ACT.Square, scale=0.5, accum_out=squares[:, t, LAST : LAST + 1]
-            )
-
-        def factor(t):
-            mine = slice(t, t + 1)
-            nc.vector.scalar_tensor_tensor(
-                out=mean_sq[:, mine],
-                in0=squares[:, t, LAST : LAST + 1],
-                scalar=1.0 / CHANNELS,
-                in1=first_sums[:, mine],
-                op0=ALU.mult,
-                op1=ALU.add,
-            )
-            nc.gpsimd.tensor_tensor(out=rstd[:, mine], in0=mean_sq[:, mine], in1=minus_half[:, mine], op=ALU.pow)
-
-
-        def scale_and_store(t, j, part=0, parts=1):
-            first = j * BLOCK_CH + part * BLOCK_CH // parts
-            columns = slice(first, first + BLOCK_CH // parts)
-            nc.vector.scalar_tensor_tensor(
-                out=blended[:, t, columns],
-                in0=blended[:, t, columns],
-                scalar=rstd[:, t : t + 1],
-                in1=norm_w_all[:, columns],
-                op0=ALU.mult,
-                op1=ALU.mult,
-            )
-            nc.sync.dma_start(out=out[t * P : (t + 1) * P, columns], in_=blended[:, t, columns])
-
+        times_gate(3, first_tokens)
+        transpose_back(3, TAGS["T3"], [0])
         square_last(0)
+        root(0)
+        take_out(0)
+        times_c(3, second_tokens)
+        plus_skip_term(3, second_tokens)
+        times_gate(3, second_tokens)
         factor(0)
-        nc.vector.tensor_scalar_mul(out=last_columns(0), in0=back_banks[LAST][0][:], scalar1=0.5)
+        transpose_back(3, TAGS["T3"], [1])
         square_last(1)
-        nc.scalar.activation(out=last_columns(1), in_=back_banks[LAST][1][:], func=ACT.Copy, scale=0.5)
+        root(1)
+        take_out(1)
+
         scale_and_store(0, 0, 0, 2)
-        factor(1)
         scale_and_store(0, 0, 1, 2)
-        for j in range(1, BLOCKS):
+        scale_and_store(0, 1)
+        factor(1)
+        for j in range(2, BLOCKS):
             scale_and_store(0, j)
         for j in range(BLOCKS):
             scale_and_store(1, j)

@@ -219,6 +219,15 @@ def tile_mamba2backbone_pb_kernel(
                 out=x_codes[:, g, :].bitcast(FP8X4), scales=x_planes[:, g, :], in_=x_grouped[:, g, :]
             )
 
+        warm = keep.tile([P, 512], BF16)
+        nc.vector.memset(warm[:], 0.0)
+
+        def keep_clock_up(n):
+            bank = psum.tile([P, 512], F32, tag="C", name="unread_bank")
+            for k in range(n):
+                nc.tensor.matmul(bank[:], lhsT=warm[:, 0:P], rhs=warm[:], start=True, stop=True)
+
+        keep_clock_up(6)
         pairs = [psum.tile([P, 2, TOKENS], F32, tag="AABB"[g], name="pairs") for g in range(GROUPS)]
         for t in range(TOKEN_TILES):
             for g in range(GROUPS):
@@ -431,33 +440,36 @@ def tile_mamba2backbone_pb_kernel(
                     op1=ALU.mult,
                 )
 
-        def transpose_back(j, tag, token_tiles=range(TOKEN_TILES)):
-            back_banks.setdefault(j, [])
+        def lay_deter(j, tag):
+            back_banks[j] = [psum.tile([P, BLOCK_CH], F32, tag=tag, name="back") for t in range(TOKEN_TILES)]
+            for t in range(TOKEN_TILES):
+                nc.tensor.matmul(
+                    back_banks[j][t][:],
+                    lhsT=two_ident[:],
+                    rhs=deter_rows[:, t, j * BLOCK_CH : (j + 1) * BLOCK_CH],
+                    start=True,
+                    stop=False,
+                )
+
+        def transpose_onto(j, token_tiles=range(TOKEN_TILES)):
             for t in token_tiles:
-                back = psum.tile([P, BLOCK_CH], F32, tag=tag, name="back")
-                if j in SCALAR_EMPTIES:
-                    nc.tensor.matmul(
-                        back[:],
-                        lhsT=two_ident[:],
-                        rhs=deter_rows[:, t, j * BLOCK_CH : (j + 1) * BLOCK_CH],
-                        start=True,
-                        stop=False,
-                    )
                 for i in range(BLOCK_TILES):
-                    part = back[:, i * P : (i + 1) * P]
-                    turned = chain[j][:, i, t * P : (t + 1) * P]
-                    if j in SCALAR_EMPTIES:
-                        nc.tensor.matmul(
-                            part,
-                            lhsT=turned,
-                            rhs=ident_f32[:],
-                            is_transpose=True,
-                            start=False,
-                            stop=(i == BLOCK_TILES - 1),
-                        )
-                    else:
-                        nc.tensor.transpose(part, turned, ident_f32[:])
-                back_banks[j].append(back)
+                    nc.tensor.matmul(
+                        back_banks[j][t][:, i * P : (i + 1) * P],
+                        lhsT=chain[j][:, i, t * P : (t + 1) * P],
+                        rhs=ident_f32[:],
+                        is_transpose=True,
+                        start=False,
+                        stop=(i == BLOCK_TILES - 1),
+                    )
+
+        def transpose_back(j, tag):
+            back_banks[j] = [psum.tile([P, BLOCK_CH], F32, tag=tag, name="back") for t in range(TOKEN_TILES)]
+            for t in range(TOKEN_TILES):
+                for i in range(BLOCK_TILES):
+                    nc.tensor.transpose(
+                        back_banks[j][t][:, i * P : (i + 1) * P], chain[j][:, i, t * P : (t + 1) * P], ident_f32[:]
+                    )
 
         def block_columns(j, t):
             return blended[:, t, j * BLOCK_CH : (j + 1) * BLOCK_CH]
@@ -525,7 +537,12 @@ def tile_mamba2backbone_pb_kernel(
             {"dt": dt_banks, "b": b_banks, "c": c_banks, "z": z_banks}[name][j] = multiply(name, j, tag)
 
         TAGS = dict(b0="A", dt0="C", dt1="D", c0="B", z0="A", dt2="C", b1="B", dt3="D", T0="A", c1="B", z1="A", b2="B", c2="C", T1="A", z2="D", b3="B", c3="C", T2="A", z3="D", T3="C")
-        def TB(j): transpose_back(j, TAGS["T" + str(j)])
+        def TB(j):
+            if j in SCALAR_EMPTIES:
+                lay_deter(j, TAGS["T" + str(j)])
+                transpose_onto(j)
+            else:
+                transpose_back(j, TAGS["T" + str(j)])
 
         product("dt", 0)
         softplus_exp(0)
@@ -630,7 +647,8 @@ def tile_mamba2backbone_pb_kernel(
             out=first_sums[:], in0=first_sums[:], scalar1=1.0 / CHANNELS, scalar2=EPS, op0=ALU.mult, op1=ALU.add
         )
         times_gate(3, first_tokens)
-        transpose_back(3, TAGS["T3"], [0])
+        lay_deter(3, TAGS["T3"])
+        transpose_onto(3, [0])
         square_last(0)
         root(0)
         take_out(0)
@@ -638,7 +656,7 @@ def tile_mamba2backbone_pb_kernel(
         plus_skip_term(3, second_tokens)
         times_gate(3, second_tokens)
         factor(0)
-        transpose_back(3, TAGS["T3"], [1])
+        transpose_onto(3, [1])
         square_last(1)
         root(1)
         take_out(1)

@@ -536,7 +536,7 @@ def tile_mamba2backbone_pb_kernel(
             tag = TAGS[name + str(j)]
             {"dt": dt_banks, "b": b_banks, "c": c_banks, "z": z_banks}[name][j] = multiply(name, j, tag)
 
-        TAGS = dict(b0="A", dt0="C", dt1="D", c0="B", z0="A", dt2="C", b1="B", dt3="D", T0="A", c1="B", z1="A", b2="B", c2="C", T1="A", z2="D", b3="B", c3="C", T2="A", z3="D", T3="C")
+        TAGS = dict(b0="A", dt0="C", dt1="D", c0="B", z0="A", dt2="C", b1="B", dt3="D", T0="A", c1="B", z1="A", b2="B", c2="C", T1="A", z2="D", b3="B", c3="C", T2="A", z3="D", T3="D")
         def TB(j):
             if j in SCALAR_EMPTIES:
                 lay_deter(j, TAGS["T" + str(j)])
@@ -642,12 +642,12 @@ def tile_mamba2backbone_pb_kernel(
         nc.vector.tensor_reduce(out=first_sums[:], in_=squares[:, :, :LAST], axis=mybir.AxisListType.X, op=ALU.add)
         tanh_z(3)
         nc.scalar.activation(out=mean_sq[:, 0:1], in_=one[:], func=ACT.Sqrt)
+        lay_deter(3, TAGS["T3"])
         plus_skip_term(3, first_tokens)
         nc.vector.tensor_scalar(
             out=first_sums[:], in0=first_sums[:], scalar1=1.0 / CHANNELS, scalar2=EPS, op0=ALU.mult, op1=ALU.add
         )
         times_gate(3, first_tokens)
-        lay_deter(3, TAGS["T3"])
         transpose_onto(3, [0])
         square_last(0)
         root(0)

@@ -429,8 +429,8 @@ def tile_mamba2backbone_pb_kernel(
                     op=ALU.add,
                 )
 
-        def times_gate(j, tokens=ALL_TOKENS):
-            for mine, whole in half_slices(j):
+        def times_gate(j, tokens=ALL_TOKENS, halves=slice(0, HALVES)):
+            for mine, whole in half_slices(j)[halves]:
                 nc.vector.scalar_tensor_tensor(
                     out=chain[j][:, mine, tokens],
                     in0=gate[j][:, mine, tokens],
@@ -554,9 +554,9 @@ def tile_mamba2backbone_pb_kernel(
         nc.scalar.activation(out=soft_a[:], in_=soft_a[:], func=ACT.Ln, bias=one[:])
         softplus_log(0)
         nc.vector.tensor_tensor(out=soft_a[:], in0=soft_a[:], in1=a_base_cols, op=ALU.max)
+        softplus_max(0)
         nc.vector.tensor_scalar_mul(out=a_neg[:], in0=soft_a[:], scalar1=-1.0)
         nc.vector.tensor_scalar_mul(out=a_dt_min[:], in0=soft_a[:], scalar1=-DT_MIN)
-        softplus_max(0)
         skip_term(1)
         skip_term(2)
         decay_exp(0)
@@ -654,8 +654,9 @@ def tile_mamba2backbone_pb_kernel(
         take_out(0)
         times_c(3, second_tokens)
         plus_skip_term(3, second_tokens)
-        times_gate(3, second_tokens)
+        times_gate(3, second_tokens, slice(0, 1))
         factor(0)
+        times_gate(3, second_tokens, slice(1, 2))
         transpose_onto(3, [1])
         square_last(1)
         root(1)
@@ -664,8 +665,8 @@ def tile_mamba2backbone_pb_kernel(
         scale_and_store(0, 0, 0, 2)
         scale_and_store(0, 0, 1, 2)
         scale_and_store(0, 1)
+        scale_and_store(0, 2)
         factor(1)
-        for j in range(2, BLOCKS):
-            scale_and_store(0, j)
+        scale_and_store(0, 3)
         for j in range(BLOCKS):
             scale_and_store(1, j)

from contextlib import ExitStack

import concourse.mybir as mybir
from concourse.masks import make_identity

F32 = mybir.dt.float32
BF16 = mybir.dt.bfloat16
I32 = mybir.dt.int32
U32 = mybir.dt.uint32
U8 = mybir.dt.uint8
FP8X4 = mybir.dt.float8_e4m3fn_x4
ACT = mybir.ActivationFunctionType
ALU = mybir.AluOpType

P = 128
PACK = 4
TOKENS = 256
TOKEN_TILES = TOKENS // P
CHANNELS = 2048
GROUPS = CHANNELS // (P * PACK)
CH_TILES = CHANNELS // P
BLOCK_TILES = 4
BLOCKS = CH_TILES // BLOCK_TILES
BLOCK_CH = BLOCK_TILES * P
HALF_TILES = 2
HALVES = BLOCK_TILES // HALF_TILES
LOG_STAYS = ((0,), (1,), (2, 3))
SCALAR_EMPTIES = (1, 2, 3)
WORDS_PER_GROUP = P * PACK // 2

WEIGHT_BUFS = 12
DT_BANKS = 4
ACC_BANKS = 4

DT_MIN = 1e-4
EPS = 1e-4
LN_MAX = 1e18

DT_B, B_B, C_B, Z_B, A_BASE, SKIP = 0, 1, 2, 3, 4, 5
VECTOR_ROWS = 6 * CH_TILES

FLOPS = 2 * TOKENS * CHANNELS * CHANNELS * 4


def tile_mamba2backbone_pb_kernel(
    tc,
    x,
    deter,
    a_base,
    dt_w_words,
    dt_w_scales,
    dt_b,
    b_w_words,
    b_w_scales,
    b_b,
    c_w_words,
    c_w_scales,
    c_b,
    z_w_words,
    z_w_scales,
    z_b,
    skip,
    norm_w,
    out,
):
    nc = tc.nc
    weight_words = {"dt": dt_w_words, "b": b_w_words, "c": c_w_words, "z": z_w_words}
    weight_scales = {"dt": dt_w_scales, "b": b_w_scales, "c": c_w_scales, "z": z_w_scales}
    weight_index = {"dt": 0, "b": 1, "c": 2, "z": 3}

    pieces = [("dt", 0), ("b", 0), ("dt", 1), ("c", 0), ("z", 0), ("dt", 2), ("b", 1), ("dt", 3), ("c", 1), ("z", 1)]
    for j in (2, 3):
        for name in ("b", "c", "z"):
            pieces.append((name, j))

    with ExitStack() as stack:
        stack.enter_context(tc.manual_schedule())
        keep = stack.enter_context(tc.tile_pool(name="keep", bufs=1))
        weights = stack.enter_context(tc.tile_pool(name="weights", bufs=WEIGHT_BUFS))
        work = stack.enter_context(tc.tile_pool(name="work", bufs=2))
        psum = stack.enter_context(tc.psum_pool(name="psum", bufs=2))

        ident_bf16 = keep.tile([P, P], BF16)
        ident_f32 = keep.tile([P, P], F32)
        vector_rows = keep.tile([P, P], BF16)
        per_channel = keep.tile([P, P], F32)
        half_z_b = keep.tile([P, CH_TILES], F32)
        soft_a = keep.tile([P, CH_TILES], F32)
        a_neg = keep.tile([P, CH_TILES], F32)
        a_dt_min = keep.tile([P, CH_TILES], F32)
        one = keep.tile([P, 1], F32)
        neg_ident = keep.tile([P, P], BF16)
        skip_cols = keep.tile([P, CH_TILES], F32)
        skip_diag = keep.tile([P, 4, P], BF16)
        first_sums = keep.tile([P, TOKEN_TILES], F32)
        two_ident = keep.tile([P, P], BF16)
        x_rows = keep.tile([P, TOKEN_TILES, CHANNELS], BF16)
        deter_rows = keep.tile([P, TOKEN_TILES, CHANNELS], BF16)
        x_grouped = keep.tile([P, GROUPS, TOKENS * PACK], BF16, align_bytes=64)
        x_codes = keep.tile([P, GROUPS, TOKENS], U32, align_bytes=64)
        x_planes = keep.tile([P, GROUPS, TOKENS], U8, align_bytes=64)
        w_planes = keep.tile([P, len(weight_index), CHANNELS], U8, align_bytes=64)
        x_t = keep.tile([P, CH_TILES, TOKENS], BF16)
        deter_t = keep.tile([P, CH_TILES, TOKENS], BF16)
        skip_x = keep.tile([P, 12, TOKENS], F32)
        blended = keep.tile([P, TOKEN_TILES, CHANNELS], F32)
        norm_w_all = keep.tile([P, CHANNELS], BF16)
        squares = keep.tile([P, TOKEN_TILES, BLOCKS], F32)
        mean_sq = keep.tile([P, TOKEN_TILES], F32)
        rstd = keep.tile([P, TOKEN_TILES], F32)

        def channel_scalar(vector, ct):
            column = CH_TILES * vector + ct
            return per_channel[:, column : column + 1]

        for v, vector in enumerate((dt_b, b_b, c_b, z_b, a_base, skip)):
            nc.scalar.dma_start(
                out=vector_rows[CH_TILES * v : CH_TILES * (v + 1), :],
                in_=vector.rearrange("(r c) -> r c", c=P),
            )
        nc.vector.memset(vector_rows[VECTOR_ROWS:P, :], 0.0)

        nc.vector.memset(w_planes[:].bitcast(I32), 0)
        nc.vector.memset(one[:], 1.0)
        nc.scalar.activation(out=rstd[:, 0:1], in_=one[:], func=ACT.Exp)

        piece_tiles = {}

        LAST = BLOCKS - 1
        LAST_PIECE = len(pieces) - 1
        IN_HALVES = (0, LAST_PIECE)
        LOADS = len(pieces)

        def load_half_piece(k, h):
            name, j = pieces[k]
            by_partition = weight_words[name].rearrange("g p n t -> p g (n t)")
            half = weights.tile([P, GROUPS, HALF_TILES * P], U32, align_bytes=64, tag="piece", name="half_piece")
            first = PACK * (BLOCK_CH * j + HALF_TILES * P * h)
            nc.sync.dma_start(
                out=half[:].bitcast(I32), in_=by_partition[:, :, first : first + PACK * HALF_TILES * P].bitcast(I32)
            )
            piece_tiles[k].append(half)

        def load_piece(k):
            name, j = pieces[k]
            if j == 0:
                for quadrant in range(4):
                    queue, word = (nc.gpsimd, F32) if name in ("b", "c", "z") else (nc.sync, I32)
                    queue.dma_start(
                        out=w_planes[32 * quadrant : 32 * quadrant + 16, weight_index[name], :].bitcast(word),
                        in_=weight_scales[name][:, 4 * quadrant : 4 * quadrant + 4, :].bitcast(word),
                    )
            if k in IN_HALVES:
                piece_tiles[k] = []
                for h in range(HALVES):
                    load_half_piece(k, h)
                return
            piece = weights.tile([P, GROUPS, BLOCK_CH], U32, align_bytes=64, tag="piece", name="piece")
            by_partition = weight_words[name].rearrange("g p n t -> p g (n t)")
            nc.sync.dma_start(
                out=piece[:].bitcast(I32),
                in_=by_partition[:, :, PACK * BLOCK_CH * j : PACK * BLOCK_CH * (j + 1)].bitcast(I32),
            )
            piece_tiles[k] = piece

        make_identity(nc, ident_f32[:])
        make_identity(nc, ident_bf16[:])
        for t in range(TOKEN_TILES):
            nc.sync.dma_start(out=x_rows[:, t, :], in_=x[t * P : (t + 1) * P, :])
        load_piece(0)
        for t in range(TOKEN_TILES):
            nc.sync.dma_start(out=deter_rows[:, t, :], in_=deter[t * P : (t + 1) * P, :])
        for k in range(1, WEIGHT_BUFS):
            load_piece(k)

        nc.vector.tensor_scalar_mul(out=two_ident[:], in0=ident_bf16[:], scalar1=2.0)
        nc.vector.tensor_scalar_mul(out=neg_ident[:], in0=ident_bf16[:], scalar1=-1.0)

        def multiply(name, j, tag):
            k = pieces.index((name, j))
            piece = piece_tiles[k]
            banks = []
            for h in range(HALVES):
                bank = psum.tile([P, HALF_TILES, TOKENS], F32, tag=tag, name="bank")
                for i in range(HALF_TILES):
                    local = (h * HALF_TILES + i) * P
                    channel = j * BLOCK_CH + local
                    for g in range(GROUPS):
                        nc.tensor.matmul_mx(
                            out=bank[:, i, :],
                            lhsT=(
                                piece[h][:, g, i * P : (i + 1) * P] if k in IN_HALVES else piece[:, g, local : local + P]
                            ).bitcast(FP8X4),
                            lhsT_scale=w_planes[4 * g : P, weight_index[name], channel : channel + P],
                            rhs=x_codes[:, g, :].bitcast(FP8X4),
                            rhs_scale=x_planes[:, g, :],
                            start=(g == 0),
                            stop=(g == GROUPS - 1),
                        )
                banks.append(bank)
            if k + WEIGHT_BUFS < LOADS:
                load_piece(k + WEIGHT_BUFS)
            return banks

        def tiles_of(j):
            return [(i, i // HALF_TILES, i % HALF_TILES, j * BLOCK_TILES + i) for i in range(BLOCK_TILES)]

        def half_slices(j):
            return [
                (
                    slice(h * HALF_TILES, (h + 1) * HALF_TILES),
                    slice(j * BLOCK_TILES + h * HALF_TILES, j * BLOCK_TILES + (h + 1) * HALF_TILES),
                )
                for h in range(HALVES)
            ]

        def quantise(g):
            nc.vector.quantize_mx(
                out=x_codes[:, g, :].bitcast(FP8X4), scales=x_planes[:, g, :], in_=x_grouped[:, g, :]
            )

        warm = keep.tile([P, 512], BF16)
        nc.vector.memset(warm[:], 0.0)

        def keep_clock_up(n):
            bank = psum.tile([P, 512], F32, tag="C", name="unread_bank")
            for k in range(n):
                nc.tensor.matmul(bank[:], lhsT=warm[:, 0:P], rhs=warm[:], start=True, stop=True)

        keep_clock_up(6)
        pairs = [psum.tile([P, 2, TOKENS], F32, tag="AABB"[g], name="pairs") for g in range(GROUPS)]
        for t in range(TOKEN_TILES):
            for g in range(GROUPS):
                for u in range(2):
                    nc.tensor.transpose(
                        pairs[g][:, u, t * P : (t + 1) * P],
                        x_rows[:, t, :].bitcast(F32)[
                            :, WORDS_PER_GROUP * g + u : WORDS_PER_GROUP * (g + 1) : 2
                        ],
                        ident_f32[:],
                    )
        def group_words(g, copy):
            copy(
                out=x_grouped[:, g, :].bitcast(F32).rearrange("p (r u) -> p r u", u=2),
                in_=pairs[g][:].rearrange("p u r -> p r u"),
            )

        group_words(0, nc.vector.tensor_copy)
        group_words(1, nc.scalar.copy)
        group_words(2, nc.vector.tensor_copy)
        group_words(3, nc.scalar.copy)
        for g in range(GROUPS):
            quantise(g)

        vector_cols = psum.tile([P, P], BF16, tag="C", name="vector_cols")
        nc.tensor.transpose(vector_cols[:], vector_rows[:], ident_bf16[:])
        nc.scalar.copy(out=per_channel[:], in_=vector_cols[:])
        a_base_cols = per_channel[:, CH_TILES * A_BASE : CH_TILES * (A_BASE + 1)]
        nc.scalar.activation(out=soft_a[:], in_=a_base_cols, func=ACT.Exp)

        nc.vector.tensor_scalar_mul(
            out=half_z_b[:], in0=per_channel[:, CH_TILES * Z_B : CH_TILES * (Z_B + 1)], scalar1=0.5
        )
        nc.vector.tensor_scalar_min(out=soft_a[:], in0=soft_a[:], scalar1=LN_MAX)
        nc.vector.tensor_copy(out=skip_cols[:], in_=per_channel[:, CH_TILES * SKIP : CH_TILES * (SKIP + 1)])
        for i in range(4):
            nc.gpsimd.tensor_scalar(
                out=skip_diag[:, i, :],
                in0=ident_bf16[:],
                scalar1=skip_cols[:, 12 + i : 12 + i + 1],
                scalar2=0.0,
                op0=ALU.mult,
                op1=ALU.add,
            )

        def transpose_rows(rows, pair):
            flipped = psum.tile([P, HALF_TILES, TOKENS], BF16, tag=FLIP_TAGS[rows is deter_rows][pair], name="flipped")
            for i in range(HALF_TILES):
                ct = pair * HALF_TILES + i
                for t in range(TOKEN_TILES):
                    nc.tensor.transpose(
                        flipped[:, i, t * P : (t + 1) * P], rows[:, t, ct * P : (ct + 1) * P], ident_bf16[:]
                    )
            return flipped

        FLIP_TAGS = ("DDAABBDD", "AABBAABB")

        def flip(rows, rows_t, pairs_of_tiles):
            for pair in pairs_of_tiles:
                flipped = transpose_rows(rows, pair)
                if pair % 2 == 0 and rows is x_rows:
                    nc.scalar.copy(out=rows_t[:, pair * HALF_TILES : (pair + 1) * HALF_TILES, :], in_=flipped[:])
                else:
                    nc.vector.tensor_copy(out=rows_t[:, pair * HALF_TILES : (pair + 1) * HALF_TILES, :], in_=flipped[:])

        flip(x_rows, x_t, range(CH_TILES // HALF_TILES))

        dt_banks, b_banks, c_banks, z_banks, back_banks = {}, {}, {}, {}, {}
        soft, decay, chain, gate = {}, {}, {}, {}

        def softplus_exp(j):
            soft[j] = work.tile([P, BLOCK_TILES, TOKENS], F32, tag="soft", bufs=BLOCKS, name="soft")
            for i, h, ih, ct in tiles_of(j):
                nc.scalar.activation(
                    out=soft[j][:, i, :], in_=dt_banks[j][h][:, ih, :], func=ACT.Exp, bias=channel_scalar(DT_B, ct)
                )

        def softplus_cut(j, halves=slice(0, HALVES)):
            for mine, whole in half_slices(j)[halves]:
                nc.vector.tensor_scalar_min(out=soft[j][:, mine, :], in0=soft[j][:, mine, :], scalar1=LN_MAX)

        def softplus_log(j):
            for mine, whole in half_slices(j):
                nc.scalar.activation(out=soft[j][:, mine, :], in_=soft[j][:, mine, :], func=ACT.Ln, bias=one[:])

        def softplus_max(j):
            for i, h, ih, ct in tiles_of(j):
                nc.vector.scalar_tensor_tensor(
                    out=soft[j][:, i, :],
                    in0=dt_banks[j][h][:, ih, :],
                    scalar=channel_scalar(DT_B, ct),
                    in1=soft[j][:, i, :],
                    op0=ALU.add,
                    op1=ALU.max,
                )

        def decay_exp(j):
            decay[j] = work.tile([P, BLOCK_TILES, TOKENS], F32, tag="decay", name="decay")
            for i, h, ih, ct in tiles_of(j):
                nc.scalar.activation(
                    out=decay[j][:, i, :],
                    in_=soft[j][:, i, :],
                    func=ACT.Exp,
                    scale=a_neg[:, ct : ct + 1],
                    bias=a_dt_min[:, ct : ct + 1],
                )

        def skip_term(j):
            for i, h, ih, ct in tiles_of(j):
                nc.vector.scalar_tensor_tensor(
                    out=skip_x[:, ct, :],
                    in0=x_t[:, ct, :],
                    scalar=channel_scalar(SKIP, ct),
                    in1=deter_t[:, ct, :],
                    op0=ALU.mult,
                    op1=ALU.subtract,
                )

        skip_banks = {}

        def skip_product(j):
            skip_banks[j] = []
            for h in range(HALVES):
                bank = psum.tile([P, HALF_TILES, TOKENS], F32, tag="B", name="skip_bank")
                for ih in range(HALF_TILES):
                    ct = j * BLOCK_TILES + h * HALF_TILES + ih
                    nc.tensor.matmul(
                        bank[:, ih, :], lhsT=skip_diag[:, ct - 12, :], rhs=x_t[:, ct, :], start=True, stop=False
                    )
                    nc.tensor.matmul(bank[:, ih, :], lhsT=neg_ident[:], rhs=deter_t[:, ct, :], start=False, stop=True)
                skip_banks[j].append(bank)

        def tanh_b(j):
            chain[j] = work.tile([P, BLOCK_TILES, TOKENS], F32, tag="chain", name="chain")
            for i, h, ih, ct in tiles_of(j):
                nc.scalar.activation(
                    out=chain[j][:, i, :], in_=b_banks[j][h][:, ih, :], func=ACT.Tanh, bias=channel_scalar(B_B, ct)
                )

        def tanh_z(j):
            gate[j] = work.tile([P, BLOCK_TILES, TOKENS], F32, tag="gate", name="gate")
            for i, h, ih, ct in tiles_of(j):
                nc.scalar.activation(
                    out=gate[j][:, i, :],
                    in_=z_banks[j][h][:, ih, :],
                    func=ACT.Tanh,
                    scale=0.5,
                    bias=half_z_b[:, ct : ct + 1],
                )

        def decay_times_deter(j):
            for mine, whole in half_slices(j):
                nc.vector.tensor_tensor(
                    out=decay[j][:, mine, :], in0=decay[j][:, mine, :], in1=deter_t[:, whole, :], op=ALU.mult
                )

        def b_times_x(j):
            for mine, whole in half_slices(j):
                nc.vector.tensor_tensor(
                    out=chain[j][:, mine, :], in0=chain[j][:, mine, :], in1=x_t[:, whole, :], op=ALU.mult
                )

        def times_dt(j):
            for mine, whole in half_slices(j):
                nc.vector.scalar_tensor_tensor(
                    out=chain[j][:, mine, :],
                    in0=soft[j][:, mine, :],
                    scalar=DT_MIN,
                    in1=chain[j][:, mine, :],
                    op0=ALU.add,
                    op1=ALU.mult,
                )

        def new_state(j):
            for mine, whole in half_slices(j):
                nc.vector.tensor_tensor(
                    out=chain[j][:, mine, :], in0=chain[j][:, mine, :], in1=decay[j][:, mine, :], op=ALU.add
                )

        ALL_TOKENS = slice(0, TOKENS)

        def times_c(j, tokens=ALL_TOKENS):
            for i, h, ih, ct in tiles_of(j):
                nc.vector.scalar_tensor_tensor(
                    out=chain[j][:, i, tokens],
                    in0=c_banks[j][h][:, ih, tokens],
                    scalar=channel_scalar(C_B, ct),
                    in1=chain[j][:, i, tokens],
                    op0=ALU.add,
                    op1=ALU.mult,
                )

        def plus_skip_term(j, tokens=ALL_TOKENS):
            for h, (mine, whole) in enumerate(half_slices(j)):
                nc.vector.tensor_tensor(
                    out=chain[j][:, mine, tokens],
                    in0=chain[j][:, mine, tokens],
                    in1=(skip_banks[j][h][:] if j in skip_banks else skip_x[:, whole, :])[:, :, tokens],
                    op=ALU.add,
                )

        def times_gate(j, tokens=ALL_TOKENS, halves=slice(0, HALVES)):
            for mine, whole in half_slices(j)[halves]:
                nc.vector.scalar_tensor_tensor(
                    out=chain[j][:, mine, tokens],
                    in0=gate[j][:, mine, tokens],
                    scalar=1.0,
                    in1=chain[j][:, mine, tokens],
                    op0=ALU.add,
                    op1=ALU.mult,
                )

        def lay_deter(j, tag):
            back_banks[j] = [psum.tile([P, BLOCK_CH], F32, tag=tag, name="back") for t in range(TOKEN_TILES)]
            for t in range(TOKEN_TILES):
                nc.tensor.matmul(
                    back_banks[j][t][:],
                    lhsT=two_ident[:],
                    rhs=deter_rows[:, t, j * BLOCK_CH : (j + 1) * BLOCK_CH],
                    start=True,
                    stop=False,
                )

        def transpose_onto(j, token_tiles=range(TOKEN_TILES)):
            for t in token_tiles:
                for i in range(BLOCK_TILES):
                    nc.tensor.matmul(
                        back_banks[j][t][:, i * P : (i + 1) * P],
                        lhsT=chain[j][:, i, t * P : (t + 1) * P],
                        rhs=ident_f32[:],
                        is_transpose=True,
                        start=False,
                        stop=(i == BLOCK_TILES - 1),
                    )

        def transpose_back(j, tag):
            back_banks[j] = [psum.tile([P, BLOCK_CH], F32, tag=tag, name="back") for t in range(TOKEN_TILES)]
            for t in range(TOKEN_TILES):
                for i in range(BLOCK_TILES):
                    nc.tensor.transpose(
                        back_banks[j][t][:, i * P : (i + 1) * P], chain[j][:, i, t * P : (t + 1) * P], ident_f32[:]
                    )

        def block_columns(j, t):
            return blended[:, t, j * BLOCK_CH : (j + 1) * BLOCK_CH]

        def blend(j):
            for t in range(TOKEN_TILES):
                if j in SCALAR_EMPTIES:
                    nc.scalar.activation(out=block_columns(j, t), in_=back_banks[j][t][:], func=ACT.Copy, scale=0.5)
                else:
                    nc.vector.scalar_tensor_tensor(
                        out=block_columns(j, t),
                        in0=back_banks[j][t][:],
                        scalar=0.5,
                        in1=deter_rows[:, t, j * BLOCK_CH : (j + 1) * BLOCK_CH],
                        op0=ALU.mult,
                        op1=ALU.add,
                    )

        def sum_squares(j):
            for t in range(TOKEN_TILES):
                unread = work.tile([P, BLOCK_CH], F32, tag="unread", name="unread")
                nc.scalar.activation(
                    out=unread[:], in_=block_columns(j, t), func=ACT.Square, accum_out=squares[:, t, j : j + 1]
                )

        def last_columns(t):
            return blended[:, t, LAST * BLOCK_CH : CHANNELS]

        def square_last(t):
            unread = work.tile([P, BLOCK_CH], F32, tag="unread", name="unread")
            nc.scalar.activation(
                out=unread[:], in_=back_banks[LAST][t][:], func=ACT.Square, scale=0.5, accum_out=squares[:, t, LAST : LAST + 1]
            )

        def root(t):
            nc.scalar.activation(
                out=mean_sq[:, t : t + 1],
                in_=squares[:, t, LAST : LAST + 1],
                func=ACT.Sqrt,
                scale=1.0 / CHANNELS,
                bias=first_sums[:, t : t + 1],
            )

        def factor(t):
            nc.vector.reciprocal(out=rstd[:, t : t + 1], in_=mean_sq[:, t : t + 1])

        def take_out(t):
            nc.scalar.activation(out=last_columns(t), in_=back_banks[LAST][t][:], func=ACT.Copy, scale=0.5)

        def scale_and_store(t, j, part=0, parts=1):
            first = j * BLOCK_CH + part * BLOCK_CH // parts
            columns = slice(first, first + BLOCK_CH // parts)
            nc.vector.scalar_tensor_tensor(
                out=blended[:, t, columns],
                in0=blended[:, t, columns],
                scalar=rstd[:, t : t + 1],
                in1=norm_w_all[:, columns],
                op0=ALU.mult,
                op1=ALU.mult,
            )
            nc.sync.dma_start(out=out[t * P : (t + 1) * P, columns], in_=blended[:, t, columns])

        def product(name, j):
            tag = TAGS[name + str(j)]
            {"dt": dt_banks, "b": b_banks, "c": c_banks, "z": z_banks}[name][j] = multiply(name, j, tag)

        TAGS = dict(b0="A", dt0="C", dt1="D", c0="B", z0="A", dt2="C", b1="B", dt3="D", T0="A", c1="B", z1="A", b2="B", c2="C", T1="A", z2="D", b3="B", c3="C", T2="A", z3="D", T3="D")
        def TB(j):
            if j in SCALAR_EMPTIES:
                lay_deter(j, TAGS["T" + str(j)])
                transpose_onto(j)
            else:
                transpose_back(j, TAGS["T" + str(j)])

        product("dt", 0)
        softplus_exp(0)
        softplus_cut(0, slice(0, 1))
        flip(deter_rows, deter_t, range(2))
        softplus_cut(0, slice(1, 2))
        flip(deter_rows, deter_t, range(2, 8))
        skip_term(0)
        nc.scalar.activation(out=soft_a[:], in_=soft_a[:], func=ACT.Ln, bias=one[:])
        softplus_log(0)
        nc.vector.tensor_tensor(out=soft_a[:], in0=soft_a[:], in1=a_base_cols, op=ALU.max)
        softplus_max(0)
        nc.vector.tensor_scalar_mul(out=a_neg[:], in0=soft_a[:], scalar1=-1.0)
        nc.vector.tensor_scalar_mul(out=a_dt_min[:], in0=soft_a[:], scalar1=-DT_MIN)
        skip_term(1)
        skip_term(2)
        decay_exp(0)
        product("b", 0)
        product("dt", 1)

        product("c", 0)
        tanh_b(0)
        decay_times_deter(0)
        product("z", 0)
        softplus_exp(1)
        b_times_x(0)
        softplus_cut(1)
        softplus_log(1)
        times_dt(0)
        new_state(0)
        times_c(0)
        product("dt", 2)
        softplus_max(1)
        tanh_z(0)
        decay_exp(1)
        softplus_exp(2)
        plus_skip_term(0)
        times_gate(0)
        softplus_cut(2)
        product("b", 1)
        product("dt", 3)
        TB(0)

        product("c", 1)
        tanh_b(1)
        decay_times_deter(1)
        softplus_exp(3)
        b_times_x(1)
        blend(0)
        product("z", 1)
        softplus_cut(3)
        softplus_log(2)
        softplus_log(3)
        times_dt(1)
        new_state(1)
        times_c(1)
        softplus_max(2)
        tanh_z(1)
        decay_exp(2)
        sum_squares(0)
        plus_skip_term(1)
        times_gate(1)
        softplus_max(3)
        product("b", 2)
        product("c", 2)
        TB(1)

        tanh_b(2)
        decay_times_deter(2)
        product("z", 2)
        b_times_x(2)
        product("b", 3)
        times_dt(2)
        new_state(2)
        times_c(2)
        decay_exp(3)
        blend(1)
        sum_squares(1)
        product("c", 3)
        tanh_z(2)
        plus_skip_term(2)
        times_gate(2)
        TB(2)

        tanh_b(3)
        decay_times_deter(3)
        product("z", 3)
        skip_product(3)
        nc.sync.dma_start(out=norm_w_all[:], in_=norm_w.partition_broadcast(P))
        b_times_x(3)
        times_dt(3)
        new_state(3)
        blend(2)
        sum_squares(2)
        first_tokens, second_tokens = (slice(t * P, (t + 1) * P) for t in range(TOKEN_TILES))
        times_c(3, first_tokens)
        nc.vector.tensor_reduce(out=first_sums[:], in_=squares[:, :, :LAST], axis=mybir.AxisListType.X, op=ALU.add)
        tanh_z(3)
        nc.scalar.activation(out=mean_sq[:, 0:1], in_=one[:], func=ACT.Sqrt)
        lay_deter(3, TAGS["T3"])
        plus_skip_term(3, first_tokens)
        nc.vector.tensor_scalar(
            out=first_sums[:], in0=first_sums[:], scalar1=1.0 / CHANNELS, scalar2=EPS, op0=ALU.mult, op1=ALU.add
        )
        times_gate(3, first_tokens)
        transpose_onto(3, [0])
        square_last(0)
        root(0)
        take_out(0)
        times_c(3, second_tokens)
        plus_skip_term(3, second_tokens)
        times_gate(3, second_tokens, slice(0, 1))
        factor(0)
        times_gate(3, second_tokens, slice(1, 2))
        transpose_onto(3, [1])
        square_last(1)
        root(1)
        take_out(1)

        scale_and_store(0, 0, 0, 2)
        scale_and_store(0, 0, 1, 2)
        scale_and_store(0, 1)
        scale_and_store(0, 2)
        factor(1)
        scale_and_store(0, 3)
        for j in range(BLOCKS):
            scale_and_store(1, j)
